import numpy as np
import ml_dtypes


def mxq(x, axis, fmt="e4m3"):
    dtype, down = {"e4m3": (ml_dtypes.float8_e4m3fn, 7), "e5m2": (ml_dtypes.float8_e5m2, 14)}[fmt]
    v = np.moveaxis(np.asarray(x, np.float32).astype(ml_dtypes.bfloat16).astype(np.float64), axis, -1)
    blocks = v.reshape(v.shape[:-1] + (-1, 32))
    amax = np.abs(blocks).max(-1, keepdims=True)
    byte = np.maximum(np.where(amax > 0, np.frexp(amax)[1] - 1 + 127, 0) - down, 1)
    scale = np.exp2(byte - 127.0)
    codes = (blocks / scale).astype(np.float32).astype(dtype).astype(np.float64)
    return np.moveaxis((codes * scale).reshape(v.shape), -1, axis)


WIDE = False


def mx_kscale(k):
    if not WIDE:
        return np.ones(k)
    levels = np.array([10, -10, 5, -5, 0])
    if k % 512:
        return np.exp2(np.random.permutation(np.resize(levels, k // 32))).repeat(32)
    a = np.empty((k // 512, 16))
    for p in range(k // 512):
        a[p, :8] = np.random.permutation(np.resize(levels, 8))
        for g in range(8):
            far = levels[np.abs(levels - a[p, g]) >= 10]
            a[p, g + 8] = far[np.random.randint(len(far))]
    return np.exp2(a.ravel()).repeat(32)


BF16 = ml_dtypes.bfloat16


def bf(x):
    return np.asarray(x, np.float32).astype(BF16)


def f64(x):
    return np.asarray(x).astype(np.float64)


B, F, H, C = 1024, 1024, 512, 10
EPS = 4.0 / 30.0
P_KEEP = 0.95


def setup_inputs():
    s = mx_kscale(F)
    ns = EPS / (6.0 * np.sqrt(H))
    return {"x1": bf(np.random.standard_normal((B, F)) * s),
            "x2": bf(np.random.standard_normal((B, F)) * s),
            "W1": bf(np.random.standard_normal((F, H)) / np.sqrt(F) / s[:, None]),
            "b1": bf(np.random.standard_normal(H) * 0.3),
            "W2": bf(np.random.standard_normal((F, H)) / np.sqrt(F) / s[:, None]),
            "b2": bf(np.random.standard_normal(H) * 0.3),
            "noise_std": bf(np.random.laplace(size=(B, H)) * ns),
            "rr_uniform": bf(np.random.uniform(size=H))}


def core(x1, x2, W1, b1, W2, b2, noise_std, rr_uniform):
    out1 = (mxq(f64(x1), 1, "e4m3") @ mxq(f64(W1), 0, "e4m3")) + f64(b1)
    one_norm = np.sum(np.abs(out1), axis=1)
    sensitivity = np.max(one_norm) - np.min(one_norm)
    noise_mul = sensitivity / EPS
    out1 = out1 + f64(noise_std) * noise_mul
    rr_mask = np.where(f64(rr_uniform) < P_KEEP, 1.0, 0.0)
    out1 = out1 * rr_mask
    out2 = (mxq(f64(x2), 1, "e4m3") @ mxq(f64(W2), 0, "e4m3")) + f64(b2)
    return np.minimum(out1, out2)


def e4m3fn_bytes(y):
    return np.clip(np.asarray(y, np.float64), -448.0, 448.0).astype(np.float32).astype(ml_dtypes.float8_e4m3fn).view(np.uint8)


def reference(x1, x2, W1, b1, W2, b2, noise_std, rr_uniform):
    out = core(x1, x2, W1, b1, W2, b2, noise_std, rr_uniform)
    s = np.max(np.abs(out)) / 448.0
    return out, e4m3fn_bytes(out / s)

@@ -1,0 +1,463 @@
+from contextlib import ExitStack
+
+import concourse.mybir as mybir
+from concourse.masks import make_identity
+
+F32 = mybir.dt.float32
+BF16 = mybir.dt.bfloat16
+U32 = mybir.dt.uint32
+U8 = mybir.dt.uint8
+FP8X4 = mybir.dt.float8_e4m3fn_x4
+FP8 = mybir.dt.float8_e4m3fn
+ALU = mybir.AluOpType
+ACT = mybir.ActivationFunctionType
+AX = mybir.AxisListType
+
+P = 128
+B, F, H = 1024, 1024, 512
+NT = B // P
+NG = F // 512
+NC = H // P
+NJ = NT // 2
+FLOPS = 2 * 2 * B * F * H
+CS_BUFS = 8
+PADS = 8
+
+
+def tile_splitnn_pa_kernel(tc, x1, x2, W1, b1, W2, b2, noise_std, rr_uniform, out_0, out_1):
+    nc = tc.nc
+    xs_in = (x1, x2)
+    ws_in = (W1, W2)
+
+    with ExitStack() as ctx:
+        keep = ctx.enter_context(tc.tile_pool(name="keep", bufs=1))
+        work = ctx.enter_context(tc.tile_pool(name="work", bufs=3))
+        psum = ctx.enter_context(tc.psum_pool(name="psum", bufs=2))
+        ctx.enter_context(tc.manual_schedule())
+
+        def bank(tag, bufs):
+            t = psum.tile([P, 512], F32, name="ps", tag="ps", bufs=8)
+            return t
+
+        ident = keep.tile([P, P], F32, name="ident")
+        make_identity(nc, ident[:])
+        zero = keep.tile([P, 1], F32, name="zero")
+        nc.vector.memset(zero[:], 0.0)
+        warm = keep.tile([P, 1], F32, name="warm")
+        nc.scalar.activation(out=warm[:], in_=zero[:], func=ACT.Abs)
+        vrow = keep.tile([P, P], BF16, name="vrow")
+        nc.vector.memset(vrow[:], 0.0)
+
+        nc.sync.dma_start(out=vrow[0:4, :], in_=b1.rearrange("(c p) -> c p", p=P))
+        nc.sync.dma_start(out=vrow[4:8, :], in_=b2.rearrange("(c p) -> c p", p=P))
+        nc.sync.dma_start(out=vrow[8:12, :], in_=rr_uniform.rearrange("(c p) -> c p", p=P))
+        wraw = [[None] * NG for c in range(2)]
+        xraw = [[None] * NJ for c in range(2)]
+
+        def load_w(c, g):
+            t = keep.tile([P, 4, H], BF16, name="wraw%d%d" % (c, g))
+            nc.sync.dma_start(out=t[:], in_=ws_in[c][g * 512 : (g + 1) * 512, :].rearrange("(p j) w -> p j w", j=4))
+            wraw[c][g] = t
+
+        def load_x(c, j):
+            t = keep.tile([P, 2, F], BF16, name="xraw%d%d" % (c, j))
+            nc.sync.dma_start(out=t[:], in_=xs_in[c].rearrange("(p t) k -> p t k", t=NT)[:, 2 * j : 2 * j + 2, :])
+            xraw[c][j] = t
+
+        noise = keep.tile([P, NT, H], BF16, name="noise")
+        noise_v = noise_std.rearrange("(p t) h -> p t h", t=NT)
+
+        load_w(0, 0)
+        load_w(0, 1)
+        for j in range(NJ):
+            load_x(0, j)
+        load_w(1, 0)
+        load_w(1, 1)
+        load_x(1, 0)
+        load_x(1, 1)
+        nc.sync.dma_start(out=noise[:, 0:4, :], in_=noise_v[:, 0:4, :])
+        load_x(1, 2)
+        load_x(1, 3)
+        nc.sync.dma_start(out=noise[:, 4:8, :], in_=noise_v[:, 4:8, :])
+
+        wcodes = []
+        wscales = []
+        for c in range(2):
+            wc = keep.tile([P, NG, H], U32, name="wcodes%d" % c, align_bytes=64)
+            wsc = keep.tile([P, NG, H], U8, name="wscales%d" % c, align_bytes=64)
+            wcodes.append(wc)
+            wscales.append(wsc)
+        xcodes = [[None] * NJ for c in range(2)]
+        xscales = [[None] * NJ for c in range(2)]
+        res_t = []
+        for c in range(2):
+            for j in range(NJ):
+                xcodes[c][j] = keep.tile([P, NG, 2 * P], U32, name="xcodes%d%d" % (c, j), align_bytes=64)
+                xscales[c][j] = keep.tile([P, NG, 2 * P], U8, name="xscales%d%d" % (c, j), align_bytes=64)
+        for c in range(2):
+            rt = keep.tile([P, NC, B], F32, name="rest%d" % c)
+            res_t.append(rt)
+        vrow32 = keep.tile([P, P], F32, name="vrow32")
+        vcol = keep.tile([P, 12], F32, name="vcol")
+        kcol = keep.tile([P, NC], F32, name="kcol")
+        identk = keep.tile([P, NC, P], F32, name="identk")
+        keepb = keep.tile([P, H], BF16, name="keepb")
+        norms = keep.tile([P, NT], F32, name="norms")
+        ext = keep.tile([P, 2], F32, name="ext")
+        gext = keep.tile([P, 2], F32, name="gext")
+        nmul = keep.tile([P, 1], F32, name="nmul")
+        nk = keep.tile([P, NT, H], BF16, name="nk")
+        junk_s = keep.tile([P, P], F32, name="junks")
+        junk_n = keep.tile([P, NT], F32, name="junkn")
+        am = keep.tile([P, 4], F32, name="am")
+        outs = []
+        o8 = []
+        for j in range(NJ):
+            ot = keep.tile([P, 2 * H + (PADS if j == NJ - 1 else 0)], F32, name="outs%d" % j)
+            outs.append(ot)
+            t8 = keep.tile([P, 2 * H], FP8, name="o8%d" % j)
+            o8.append(t8)
+        nc.vector.memset(outs[NJ - 1][:, 2 * H : 2 * H + PADS], 0.0)
+        out0_v = out_0.rearrange("(p t) h -> p t h", t=NT)
+        out1_v = out_1.rearrange("(p t) h -> p t h", t=NT)
+        live = {}
+
+        def vec_a():
+            nc.vector.tensor_copy(out=vrow32[:], in_=vrow[:])
+            vps = bank("bt", 3)
+            nc.tensor.transpose(vps[:, 0:P], vrow32[:], ident[:])
+            nc.vector.tensor_copy(out=vcol[:], in_=vps[:, 0:12])
+            nc.vector.tensor_scalar(out=kcol[:], in0=vcol[:, 8:12], scalar1=0.95, scalar2=None, op0=ALU.is_lt)
+            for c in range(NC):
+                nc.gpsimd.tensor_scalar(
+                    out=identk[:, c, :], in0=ident[:], scalar1=kcol[:, c : c + 1], scalar2=0.0, op0=ALU.mult, op1=ALU.add
+                )
+
+        def vec_b():
+            kps = bank("bt", 3)
+            for c in range(NC):
+                nc.tensor.transpose(kps[:, c * P : (c + 1) * P], kcol[:, c : c + 1].to_broadcast([P, P]), ident[:])
+            nc.scalar.copy(out=keepb[:], in_=kps[:])
+
+        def wi(c, g, parts):
+            wg = work.tile([P, H, 4], BF16, name="wg", tag="wg", bufs=4, align_bytes=64)
+            live["wg", c, g] = wg
+            for (e, a, b) in parts:
+                src = wraw[c][g][:, :, a:b].rearrange("p j w -> p w j")
+                if e == "s":
+                    nc.scalar.copy(out=wg[:, a:b, :], in_=src)
+                elif e == "g":
+                    nc.gpsimd.tensor_scalar(out=wg[:, a:b, :], in0=src, scalar1=1.0, scalar2=0.0, op0=ALU.mult, op1=ALU.add)
+                else:
+                    nc.vector.tensor_copy(out=wg[:, a:b, :], in_=src)
+
+        def wq(c, g):
+            nc.vector.quantize_mx(
+                out=wcodes[c][:, g, :].bitcast(FP8X4),
+                scales=wscales[c][:, g, :],
+                in_=live["wg", c, g][:].rearrange("p w j -> p (w j)"),
+            )
+
+        def xt(c, t):
+            words = xraw[c][t // 2][:, t % 2, :].bitcast(F32)
+            pt = psum.tile([P, 2 * NG, P], F32, name="ps", tag="ps", bufs=8)
+            live["xt", c, t] = pt
+            for g in range(NG):
+                for u in range(2):
+                    nc.tensor.transpose(pt[:, 2 * g + u, :], words[:, 256 * g + u : 256 * (g + 1) : 2], ident[:])
+
+        def xe(c, t, e):
+            if t % 2 == 0:
+                xg = work.tile([P, NG, 2 * P, 4], BF16, name="xg", tag="xg", bufs=4, align_bytes=64)
+                live["xg", c, t // 2] = xg
+            xg = live["xg", c, t // 2]
+            i = t % 2
+            dst = xg[:].bitcast(F32)[:, :, i * P : (i + 1) * P, :]
+            src = live["xt", c, t][:].rearrange("p (g u) r -> p g r u", g=NG)
+            if e == "s":
+                nc.scalar.copy(out=dst, in_=src)
+            else:
+                nc.vector.tensor_copy(out=dst, in_=src)
+
+        def xq(c, j):
+            nc.vector.quantize_mx(
+                out=xcodes[c][j][:].rearrange("p g r -> p (g r)").bitcast(FP8X4),
+                scales=xscales[c][j][:].rearrange("p g r -> p (g r)"),
+                in_=live["xg", c, j][:].rearrange("p g r j -> p (g r j)"),
+            )
+
+        def mm(c, js, h):
+            acc = bank("acc", 3)
+            live["acc", c, js[0], h] = acc
+            for i, j in enumerate(js):
+                for g in range(NG):
+                    nc.tensor.matmul_mx(
+                        out=acc[:, i * 256 : (i + 1) * 256],
+                        lhsT=wcodes[c][:, g, h * P : (h + 1) * P].bitcast(FP8X4),
+                        lhsT_scale=wscales[c][:, g, h * P : (h + 1) * P],
+                        rhs=xcodes[c][j][:, g, :].bitcast(FP8X4),
+                        rhs_scale=xscales[c][j][:, g, :],
+                        start=(g == 0),
+                        stop=(g == NG - 1),
+                    )
+
+        def ev(c, js, h, e):
+            acc = live["acc", c, js[0], h]
+            bias = vcol[:, 4 * c + h : 4 * c + h + 1]
+            src = acc[:, 0 : 256 * len(js)]
+            dst = res_t[c][:, h, 256 * js[0] : 256 * (js[0] + len(js))]
+            if e == "s":
+                nc.scalar.activation(out=dst, in_=src, func=ACT.Identity, bias=bias, scale=1.0)
+            else:
+                nc.vector.tensor_scalar(out=dst, in0=src, scalar1=bias, scalar2=None, op0=ALU.add)
+
+        def bt(c, t, masked):
+            pb = bank("bt", 3)
+            live["bt", c, t, masked] = pb
+            for h in range(NC):
+                nc.tensor.transpose(
+                    pb[:, h * P : (h + 1) * P],
+                    res_t[c][:, h, t * P : (t + 1) * P],
+                    identk[:, h, :] if masked else ident[:],
+                )
+
+        def absum(t):
+            junk = work.tile([P, H], BF16, name="junk", tag="junk", bufs=2)
+            nc.scalar.activation(out=junk[:], in_=live["bt", 0, t, False][:], func=ACT.Abs, accum_out=norms[:, t : t + 1])
+
+        def sens_a():
+            nc.vector.tensor_reduce(out=ext[:, 0:1], in_=norms[:], axis=AX.X, op=ALU.max)
+            nc.vector.tensor_scalar(
+                out=junk_n[:], in0=norms[:], scalar1=-1.0, scalar2=None, op0=ALU.mult, op1=ALU.max, accum_out=ext[:, 1:2]
+            )
+            pe_ = bank("bt", 3)
+            nc.tensor.transpose(pe_[:, 0:P], ext[:, 0:1].to_broadcast([P, P]), ident[:])
+            nc.tensor.transpose(pe_[:, P : 2 * P], ext[:, 1:2].to_broadcast([P, P]), ident[:])
+            nc.vector.tensor_reduce(
+                out=gext[:], in_=pe_[:, 0 : 2 * P].rearrange("p (e q) -> p e q", e=2), axis=AX.X, op=ALU.max
+            )
+            nc.vector.tensor_scalar(
+                out=nmul[:], in0=gext[:, 0:1], scalar1=gext[:, 1:2], scalar2=7.5, op0=ALU.add, op1=ALU.mult
+            )
+
+        def mask_noise(t, e):
+            if e == "g":
+                nc.gpsimd.tensor_tensor(out=nk[:, t, :], in0=noise[:, t, :], in1=keepb[:], op=ALU.mult)
+            else:
+                nc.vector.tensor_tensor(out=nk[:, t, :], in0=noise[:, t, :], in1=keepb[:], op=ALU.mult)
+
+        def stt(t):
+            cs = work.tile([P, H], F32, name="cs", tag="cs", bufs=CS_BUFS)
+            live["cs", t] = cs
+            nc.vector.scalar_tensor_tensor(
+                out=cs[:], in0=nk[:, t, :], scalar=nmul[:, 0:1], in1=live["bt", 0, t, True][:], op0=ALU.mult, op1=ALU.add
+            )
+
+        def fmin(t):
+            nc.vector.tensor_tensor(
+                out=outs[t // 2][:, (t % 2) * H : (t % 2 + 1) * H], in0=live["cs", t][:], in1=live["bt", 1, t, False][:], op=ALU.min
+            )
+
+        def amax(k, j, a, b):
+            nc.vector.tensor_reduce(
+                out=outs[NJ - 1][:, 2 * H + k : 2 * H + k + 1], in_=outs[j][:, a:b], axis=AX.X, op=ALU.max, apply_absolute_value=True
+            )
+
+        def store0(j):
+            nc.sync.dma_start(out=out0_v[:, 2 * j : 2 * j + 2, :], in_=outs[j][:, 0 : 2 * H].rearrange("p (t h) -> p t h", t=2))
+
+        def scale():
+            nc.vector.tensor_reduce(
+                out=am[:, 0:1], in_=outs[NJ - 1][:, H : 2 * H + PADS], axis=AX.X, op=ALU.max, apply_absolute_value=True
+            )
+            pa_ = bank("bt", 3)
+            nc.tensor.transpose(pa_[:, 0:P], am[:, 0:1].to_broadcast([P, P]), ident[:])
+            nc.vector.tensor_scalar(
+                out=junk_s[:], in0=pa_[:, 0:P], scalar1=1.0 / 448.0, scalar2=None, op0=ALU.mult, op1=ALU.max, accum_out=am[:, 1:2]
+            )
+            nc.vector.reciprocal(out=am[:, 2:3], in_=am[:, 1:2])
+
+        def assist(t):
+            sn = work.tile([P, H], F32, name="sn", tag="sn", bufs=2)
+            sa = work.tile([P, H], F32, name="sa", tag="sa", bufs=2)
+            cs = work.tile([P, H], F32, name="cs", tag="cs", bufs=CS_BUFS)
+            live["cs", t] = cs
+            nc.scalar.activation(out=sn[:], in_=nk[:, t, :], func=ACT.Identity, scale=nmul[:, 0:1])
+            nc.scalar.copy(out=sa[:], in_=live["bt", 0, t, True][:])
+            nc.gpsimd.tensor_tensor(out=cs[:], in0=sn[:], in1=sa[:], op=ALU.add)
+
+        def cast_v(dst, src):
+            nc.vector.tensor_scalar(out=dst, in0=src, scalar1=am[:, 2:3], scalar2=None, op0=ALU.mult, saturate=False)
+
+        def cast_s(dst, src):
+            nc.scalar.activation(out=dst, in_=src, func=ACT.Identity, scale=am[:, 2:3], bias=zero[:, 0:1], saturate=False)
+
+        def store8(j):
+            nc.sync.dma_start(out=out1_v[:, 2 * j : 2 * j + 2, :], in_=o8[j][:].bitcast(U8).rearrange("p (t h) -> p t h", t=2))
+
+        vec_a()
+        vec_b()
+        xt(0, 0)
+        wi(0, 0, (("v", 0, 512),))
+        wq(0, 0)
+        xt(0, 1)
+        wi(0, 1, (("s", 0, 192), ("v", 192, 512)))
+        wq(0, 1)
+        xe(0, 0, "s")
+        xt(0, 2)
+        xe(0, 1, "s")
+        xt(0, 3)
+        xe(0, 2, "v")
+        xt(0, 5)
+        xe(0, 3, "s")
+        xq(0, 0)
+        xq(0, 1)
+        xt(0, 4)
+        xe(0, 4, "s")
+        mask_noise(0, "g")
+        xt(0, 6)
+        mm(0, (0, 1), 3)
+        xe(0, 5, "v")
+        mm(0, (0, 1), 0)
+        mm(0, (0, 1), 1)
+        mm(0, (0, 1), 2)
+        ev(0, (0, 1), 3, "s")
+        xt(0, 7)
+        ev(0, (0, 1), 1, "s")
+        xq(0, 2)
+        ev(0, (0, 1), 0, "v")
+        xe(0, 6, "s")
+        xe(0, 7, "s")
+        ev(0, (0, 1), 2, "v")
+        wi(1, 0, (("v", 0, 512),))
+        mm(0, (2,), 1)
+        mm(0, (2,), 2)
+        xq(0, 3)
+        bt(0, 0, False)
+        ev(0, (2,), 1, "s")
+        bt(0, 1, False)
+        absum(0)
+        bt(0, 2, False)
+        absum(2)
+        absum(1)
+        mm(0, (2,), 0)
+        bt(0, 3, False)
+        ev(0, (2,), 2, "v")
+        mm(0, (2,), 3)
+        mm(0, (3,), 1)
+        ev(0, (2,), 3, "v")
+        ev(0, (3,), 1, "v")
+        mm(0, (3,), 3)
+        ev(0, (2,), 0, "s")
+        mask_noise(7, "g")
+        mm(0, (3,), 0)
+        mm(0, (3,), 2)
+        bt(0, 4, False)
+        absum(3)
+        ev(0, (3,), 3, "s")
+        ev(0, (3,), 0, "v")
+        bt(0, 5, False)
+        mask_noise(2, "g")
+        bt(0, 2, True)
+        absum(4)
+        ev(0, (3,), 2, "v")
+        mask_noise(6, "g")
+        bt(0, 6, False)
+        wq(1, 0)
+        absum(5)
+        xt(1, 1)
+        bt(0, 7, False)
+        wi(1, 1, (("v", 0, 512),))
+        xt(1, 0)
+        xt(1, 2)
+        bt(0, 0, True)
+        absum(6)
+        absum(7)
+        xe(1, 0, "s")
+        xe(1, 1, "s")
+        bt(0, 6, True)
+        wq(1, 1)
+        mask_noise(1, "g")
+        sens_a()
+        mask_noise(3, "g")
+        xt(1, 3)
+        xe(1, 2, "s")
+        bt(0, 3, True)
+        xq(1, 0)
+        xe(1, 3, "s")
+        xq(1, 1)
+        xt(1, 4)
+        xe(1, 4, "s")
+        bt(0, 7, True)
+        bt(0, 1, True)
+        stt(2)
+        xt(1, 5)
+        stt(1)
+        stt(7)
+        mm(1, (0, 1), 0)
+        xe(1, 5, "s")
+        mask_noise(5, "g")
+        stt(6)
+        ev(1, (0, 1), 0, "s")
+        bt(0, 5, True)
+        xq(1, 2)
+        mm(1, (0, 1), 1)
+        bt(0, 4, True)
+        mm(1, (0, 1), 2)
+        ev(1, (0, 1), 1, "s")
+        mask_noise(4, "g")
+        stt(3)
+        mm(1, (0, 1), 3)
+        ev(1, (0, 1), 2, "s")
+        ev(1, (0, 1), 3, "s")
+        xt(1, 6)
+        xt(1, 7)
+        stt(0)
+        xe(1, 6, "s")
+        bt(1, 0, False)
+        xe(1, 7, "s")
+        stt(5)
+        stt(4)
+        bt(1, 2, False)
+        fmin(0)
+        xq(1, 3)
+        bt(1, 3, False)
+        bt(1, 1, False)
+        fmin(1)
+        mm(1, (2, 3), 0)
+        mm(1, (2, 3), 1)
+        fmin(3)
+        fmin(2)
+        ev(1, (2, 3), 0, "s")
+        ev(1, (2, 3), 1, "s")
+        mm(1, (2, 3), 2)
+        mm(1, (2, 3), 3)
+        ev(1, (2, 3), 2, "s")
+        amax(0, 0, 0, 2 * H)
+        ev(1, (2, 3), 3, "s")
+        bt(1, 4, False)
+        amax(1, 1, 0, 2 * H)
+        store0(1)
+        bt(1, 5, False)
+        bt(1, 6, False)
+        fmin(4)
+        bt(1, 7, False)
+        store0(0)
+        fmin(5)
+        fmin(7)
+        store0(2)
+        fmin(6)
+        amax(2, 2, 0, 2 * H)
+        store0(3)
+        amax(3, 3, 0, H)
+        scale()
+        cast_v(o8[0][:], outs[0][:])
+        cast_s(o8[2][:, H : 2 * H], outs[2][:, H : 2 * H])
+        cast_s(o8[2][:, 0:H], outs[2][:, 0:H])
+        store8(0)
+        cast_s(o8[3][:, H : 2 * H], outs[3][:, H : 2 * H])
+        store8(2)
+        cast_v(o8[1][:], outs[1][:])
+        cast_v(o8[3][:, 0:H], outs[3][:, 0:H])
+        store8(1)
+        store8(3)

@@ -20,7 +20,6 @@ NG = F // 512
 NC = H // P
 NJ = NT // 2
 FLOPS = 2 * 2 * B * F * H
-CS_BUFS = 8
 PADS = 8
 
 
@@ -31,131 +30,142 @@ def tile_splitnn_pa_kernel(tc, x1, x2, W1, b1, W2, b2, noise_std, rr_uniform, ou
 
     with ExitStack() as ctx:
         keep = ctx.enter_context(tc.tile_pool(name="keep", bufs=1))
-        work = ctx.enter_context(tc.tile_pool(name="work", bufs=3))
-        psum = ctx.enter_context(tc.psum_pool(name="psum", bufs=2))
+        psum = ctx.enter_context(tc.psum_pool(name="psum", bufs=8))
         ctx.enter_context(tc.manual_schedule())
 
-        def bank(tag, bufs):
+        def bank():
             t = psum.tile([P, 512], F32, name="ps", tag="ps", bufs=8)
             return t
 
         ident = keep.tile([P, P], F32, name="ident")
-        make_identity(nc, ident[:])
         zero = keep.tile([P, 1], F32, name="zero")
-        nc.vector.memset(zero[:], 0.0)
         warm = keep.tile([P, 1], F32, name="warm")
-        nc.scalar.activation(out=warm[:], in_=zero[:], func=ACT.Abs)
         vrow = keep.tile([P, P], BF16, name="vrow")
-        nc.vector.memset(vrow[:], 0.0)
-
-        nc.sync.dma_start(out=vrow[0:4, :], in_=b1.rearrange("(c p) -> c p", p=P))
-        nc.sync.dma_start(out=vrow[4:8, :], in_=b2.rearrange("(c p) -> c p", p=P))
-        nc.sync.dma_start(out=vrow[8:12, :], in_=rr_uniform.rearrange("(c p) -> c p", p=P))
-        wraw = [[None] * NG for c in range(2)]
-        xraw = [[None] * NJ for c in range(2)]
-
-        def load_w(c, g):
-            t = keep.tile([P, 4, H], BF16, name="wraw%d%d" % (c, g))
-            nc.sync.dma_start(out=t[:], in_=ws_in[c][g * 512 : (g + 1) * 512, :].rearrange("(p j) w -> p j w", j=4))
-            wraw[c][g] = t
-
-        def load_x(c, j):
-            t = keep.tile([P, 2, F], BF16, name="xraw%d%d" % (c, j))
-            nc.sync.dma_start(out=t[:], in_=xs_in[c].rearrange("(p t) k -> p t k", t=NT)[:, 2 * j : 2 * j + 2, :])
-            xraw[c][j] = t
-
-        noise = keep.tile([P, NT, H], BF16, name="noise")
-        noise_v = noise_std.rearrange("(p t) h -> p t h", t=NT)
-
-        load_w(0, 0)
-        load_w(0, 1)
-        for j in range(NJ):
-            load_x(0, j)
-        load_w(1, 0)
-        load_w(1, 1)
-        load_x(1, 0)
-        load_x(1, 1)
-        nc.sync.dma_start(out=noise[:, 0:4, :], in_=noise_v[:, 0:4, :])
-        load_x(1, 2)
-        load_x(1, 3)
-        nc.sync.dma_start(out=noise[:, 4:8, :], in_=noise_v[:, 4:8, :])
-
-        wcodes = []
-        wscales = []
-        for c in range(2):
-            wc = keep.tile([P, NG, H], U32, name="wcodes%d" % c, align_bytes=64)
-            wsc = keep.tile([P, NG, H], U8, name="wscales%d" % c, align_bytes=64)
-            wcodes.append(wc)
-            wscales.append(wsc)
-        xcodes = [[None] * NJ for c in range(2)]
-        xscales = [[None] * NJ for c in range(2)]
-        res_t = []
-        for c in range(2):
-            for j in range(NJ):
-                xcodes[c][j] = keep.tile([P, NG, 2 * P], U32, name="xcodes%d%d" % (c, j), align_bytes=64)
-                xscales[c][j] = keep.tile([P, NG, 2 * P], U8, name="xscales%d%d" % (c, j), align_bytes=64)
-        for c in range(2):
-            rt = keep.tile([P, NC, B], F32, name="rest%d" % c)
-            res_t.append(rt)
         vrow32 = keep.tile([P, P], F32, name="vrow32")
         vcol = keep.tile([P, 12], F32, name="vcol")
         kcol = keep.tile([P, NC], F32, name="kcol")
         identk = keep.tile([P, NC, P], F32, name="identk")
         keepb = keep.tile([P, H], BF16, name="keepb")
+        noise = keep.tile([P, NT, H], BF16, name="noise")
+        nk = keep.tile([P, NT, H], BF16, name="nk")
         norms = keep.tile([P, NT], F32, name="norms")
+        junk_n = keep.tile([P, NT], F32, name="junkn")
+        junk_s = keep.tile([P, P], F32, name="junks")
         ext = keep.tile([P, 2], F32, name="ext")
         gext = keep.tile([P, 2], F32, name="gext")
         nmul = keep.tile([P, 1], F32, name="nmul")
-        nk = keep.tile([P, NT, H], BF16, name="nk")
-        junk_s = keep.tile([P, P], F32, name="junks")
-        junk_n = keep.tile([P, NT], F32, name="junkn")
         am = keep.tile([P, 4], F32, name="am")
-        outs = []
-        o8 = []
+        wraw = [[None] * NG for c in range(2)]
+        wgrp = [[None] * NG for c in range(2)]
+        xraw = [[None] * NJ for c in range(2)]
+        xgrp = [[None] * NJ for c in range(2)]
+        xcodes = [[None] * NJ for c in range(2)]
+        xscales = [[None] * NJ for c in range(2)]
+        wcodes = [None] * 2
+        wscales = [None] * 2
+        res_t = [None] * 2
+        for c in range(2):
+            wcodes[c] = keep.tile([P, NG, H], U32, name="wcodes%d" % c, align_bytes=64)
+            wscales[c] = keep.tile([P, NG, H], U8, name="wscales%d" % c, align_bytes=64)
+            res_t[c] = keep.tile([P, NC, B], F32, name="rest%d" % c)
+            for g in range(NG):
+                wraw[c][g] = keep.tile([P, 4, H], BF16, name="wraw%d%d" % (c, g))
+                wgrp[c][g] = keep.tile([P, H, 4], BF16, name="wgrp%d%d" % (c, g), align_bytes=64)
+            for j in range(NJ):
+                xraw[c][j] = keep.tile([P, 2, F], BF16, name="xraw%d%d" % (c, j))
+                xgrp[c][j] = keep.tile([P, NG, 2 * P, 4], BF16, name="xgrp%d%d" % (c, j), align_bytes=64)
+                xcodes[c][j] = keep.tile([P, NG, 2 * P], U32, name="xcodes%d%d" % (c, j), align_bytes=64)
+                xscales[c][j] = keep.tile([P, NG, 2 * P], U8, name="xscales%d%d" % (c, j), align_bytes=64)
+        junk = [None] * 2
+        for i in range(2):
+            junk[i] = keep.tile([P, H], BF16, name="junk%d" % i)
+        cs = [None] * NT
+        for t in range(NT):
+            cs[t] = keep.tile([P, H], F32, name="cs%d" % t)
+        outs = [None] * NJ
+        o8 = [None] * NJ
         for j in range(NJ):
-            ot = keep.tile([P, 2 * H + (PADS if j == NJ - 1 else 0)], F32, name="outs%d" % j)
-            outs.append(ot)
-            t8 = keep.tile([P, 2 * H], FP8, name="o8%d" % j)
-            o8.append(t8)
-        nc.vector.memset(outs[NJ - 1][:, 2 * H : 2 * H + PADS], 0.0)
+            outs[j] = keep.tile([P, 2 * H + (PADS if j == NJ - 1 else 0)], F32, name="outs%d" % j)
+            o8[j] = keep.tile([P, 2 * H], FP8, name="o8%d" % j)
         out0_v = out_0.rearrange("(p t) h -> p t h", t=NT)
         out1_v = out_1.rearrange("(p t) h -> p t h", t=NT)
+        noise_v = noise_std.rearrange("(p t) h -> p t h", t=NT)
         live = {}
 
-        def vec_a():
+        make_identity(nc, ident[:])
+        nc.vector.memset(zero[:], 0.0)
+        nc.scalar.activation(out=warm[:], in_=zero[:], func=ACT.Abs)
+        nc.vector.memset(vrow[:], 0.0)
+        nc.vector.memset(outs[NJ - 1][:, 2 * H : 2 * H + PADS], 0.0)
+        nc.sync.dma_start(out=vrow[0:4, :], in_=b1.rearrange("(c p) -> c p", p=P))
+        nc.sync.dma_start(out=vrow[4:8, :], in_=b2.rearrange("(c p) -> c p", p=P))
+        nc.sync.dma_start(out=vrow[8:12, :], in_=rr_uniform.rearrange("(c p) -> c p", p=P))
+
+        def load_w(c, g):
+            nc.sync.dma_start(
+                out=wraw[c][g][:], in_=ws_in[c][g * 512 : (g + 1) * 512, :].rearrange("(p j) w -> p j w", j=4)
+            )
+
+        def load_x(c, j):
+            nc.sync.dma_start(
+                out=xraw[c][j][:], in_=xs_in[c].rearrange("(p t) k -> p t k", t=NT)[:, 2 * j : 2 * j + 2, :]
+            )
+
+        def load_n(i):
+            nc.sync.dma_start(out=noise[:, 4 * i : 4 * i + 4, :], in_=noise_v[:, 4 * i : 4 * i + 4, :])
+
+        load_w(0, 0)
+        load_w(0, 1)
+        load_x(0, 0)
+        load_x(0, 1)
+        load_x(0, 2)
+        load_x(0, 3)
+        load_w(1, 0)
+        load_w(1, 1)
+        load_x(1, 0)
+        load_x(1, 1)
+        load_n(0)
+        load_x(1, 2)
+        load_x(1, 3)
+        load_n(1)
+
+        def va1():
             nc.vector.tensor_copy(out=vrow32[:], in_=vrow[:])
-            vps = bank("bt", 3)
-            nc.tensor.transpose(vps[:, 0:P], vrow32[:], ident[:])
-            nc.vector.tensor_copy(out=vcol[:], in_=vps[:, 0:12])
+
+        def va2():
+            live["vps"] = bank()
+            nc.tensor.transpose(live["vps"][:, 0:P], vrow32[:], ident[:])
+
+        def va3():
+            nc.vector.tensor_copy(out=vcol[:], in_=live["vps"][:, 0:12])
             nc.vector.tensor_scalar(out=kcol[:], in0=vcol[:, 8:12], scalar1=0.95, scalar2=None, op0=ALU.is_lt)
-            for c in range(NC):
+
+        def va4():
+            for h in range(NC):
                 nc.gpsimd.tensor_scalar(
-                    out=identk[:, c, :], in0=ident[:], scalar1=kcol[:, c : c + 1], scalar2=0.0, op0=ALU.mult, op1=ALU.add
+                    out=identk[:, h, :], in0=ident[:], scalar1=kcol[:, h : h + 1], scalar2=0.0, op0=ALU.mult, op1=ALU.add
                 )
 
-        def vec_b():
-            kps = bank("bt", 3)
-            for c in range(NC):
-                nc.tensor.transpose(kps[:, c * P : (c + 1) * P], kcol[:, c : c + 1].to_broadcast([P, P]), ident[:])
-            nc.scalar.copy(out=keepb[:], in_=kps[:])
+        def vb1():
+            live["kps"] = bank()
+            for h in range(NC):
+                nc.tensor.transpose(live["kps"][:, h * P : (h + 1) * P], kcol[:, h : h + 1].to_broadcast([P, P]), ident[:])
 
-        def wi(c, g, parts):
-            wg = work.tile([P, H, 4], BF16, name="wg", tag="wg", bufs=4, align_bytes=64)
-            live["wg", c, g] = wg
-            for (e, a, b) in parts:
-                src = wraw[c][g][:, :, a:b].rearrange("p j w -> p w j")
-                if e == "s":
-                    nc.scalar.copy(out=wg[:, a:b, :], in_=src)
-                elif e == "g":
-                    nc.gpsimd.tensor_scalar(out=wg[:, a:b, :], in0=src, scalar1=1.0, scalar2=0.0, op0=ALU.mult, op1=ALU.add)
-                else:
-                    nc.vector.tensor_copy(out=wg[:, a:b, :], in_=src)
+        def vb2():
+            nc.scalar.copy(out=keepb[:], in_=live["kps"][:])
+
+        def wi(c, g, e, a, b):
+            src = wraw[c][g][:, :, a:b].rearrange("p j w -> p w j")
+            if e == "s":
+                nc.scalar.copy(out=wgrp[c][g][:, a:b, :], in_=src)
+            else:
+                nc.vector.tensor_copy(out=wgrp[c][g][:, a:b, :], in_=src)
 
         def wq(c, g):
             nc.vector.quantize_mx(
                 out=wcodes[c][:, g, :].bitcast(FP8X4),
                 scales=wscales[c][:, g, :],
-                in_=live["wg", c, g][:].rearrange("p w j -> p (w j)"),
+                in_=wgrp[c][g][:].rearrange("p w j -> p (w j)"),
             )
 
         def xt(c, t):
@@ -167,12 +177,8 @@ def tile_splitnn_pa_kernel(tc, x1, x2, W1, b1, W2, b2, noise_std, rr_uniform, ou
                     nc.tensor.transpose(pt[:, 2 * g + u, :], words[:, 256 * g + u : 256 * (g + 1) : 2], ident[:])
 
         def xe(c, t, e):
-            if t % 2 == 0:
-                xg = work.tile([P, NG, 2 * P, 4], BF16, name="xg", tag="xg", bufs=4, align_bytes=64)
-                live["xg", c, t // 2] = xg
-            xg = live["xg", c, t // 2]
             i = t % 2
-            dst = xg[:].bitcast(F32)[:, :, i * P : (i + 1) * P, :]
+            dst = xgrp[c][t // 2][:].bitcast(F32)[:, :, i * P : (i + 1) * P, :]
             src = live["xt", c, t][:].rearrange("p (g u) r -> p g r u", g=NG)
             if e == "s":
                 nc.scalar.copy(out=dst, in_=src)
@@ -183,11 +189,11 @@ def tile_splitnn_pa_kernel(tc, x1, x2, W1, b1, W2, b2, noise_std, rr_uniform, ou
             nc.vector.quantize_mx(
                 out=xcodes[c][j][:].rearrange("p g r -> p (g r)").bitcast(FP8X4),
                 scales=xscales[c][j][:].rearrange("p g r -> p (g r)"),
-                in_=live["xg", c, j][:].rearrange("p g r j -> p (g r j)"),
+                in_=xgrp[c][j][:].rearrange("p g r j -> p (g r j)"),
             )
 
         def mm(c, js, h):
-            acc = bank("acc", 3)
+            acc = bank()
             live["acc", c, js[0], h] = acc
             for i, j in enumerate(js):
                 for g in range(NG):
@@ -202,39 +208,41 @@ def tile_splitnn_pa_kernel(tc, x1, x2, W1, b1, W2, b2, noise_std, rr_uniform, ou
                     )
 
         def ev(c, js, h, e):
-            acc = live["acc", c, js[0], h]
-            bias = vcol[:, 4 * c + h : 4 * c + h + 1]
-            src = acc[:, 0 : 256 * len(js)]
+            src = live["acc", c, js[0], h][:, 0 : 256 * len(js)]
             dst = res_t[c][:, h, 256 * js[0] : 256 * (js[0] + len(js))]
+            bias = vcol[:, 4 * c + h : 4 * c + h + 1]
             if e == "s":
                 nc.scalar.activation(out=dst, in_=src, func=ACT.Identity, bias=bias, scale=1.0)
             else:
                 nc.vector.tensor_scalar(out=dst, in0=src, scalar1=bias, scalar2=None, op0=ALU.add)
 
         def bt(c, t, masked):
-            pb = bank("bt", 3)
+            pb = bank()
             live["bt", c, t, masked] = pb
             for h in range(NC):
                 nc.tensor.transpose(
-                    pb[:, h * P : (h + 1) * P],
-                    res_t[c][:, h, t * P : (t + 1) * P],
-                    identk[:, h, :] if masked else ident[:],
+                    pb[:, h * P : (h + 1) * P], res_t[c][:, h, t * P : (t + 1) * P], identk[:, h, :] if masked else ident[:]
                 )
 
         def absum(t):
-            junk = work.tile([P, H], BF16, name="junk", tag="junk", bufs=2)
-            nc.scalar.activation(out=junk[:], in_=live["bt", 0, t, False][:], func=ACT.Abs, accum_out=norms[:, t : t + 1])
+            nc.scalar.activation(
+                out=junk[t % 2][:], in_=live["bt", 0, t, False][:], func=ACT.Abs, accum_out=norms[:, t : t + 1]
+            )
 
-        def sens_a():
+        def se1():
             nc.vector.tensor_reduce(out=ext[:, 0:1], in_=norms[:], axis=AX.X, op=ALU.max)
             nc.vector.tensor_scalar(
                 out=junk_n[:], in0=norms[:], scalar1=-1.0, scalar2=None, op0=ALU.mult, op1=ALU.max, accum_out=ext[:, 1:2]
             )
-            pe_ = bank("bt", 3)
-            nc.tensor.transpose(pe_[:, 0:P], ext[:, 0:1].to_broadcast([P, P]), ident[:])
-            nc.tensor.transpose(pe_[:, P : 2 * P], ext[:, 1:2].to_broadcast([P, P]), ident[:])
+
+        def se2():
+            live["eps"] = bank()
+            for i in range(2):
+                nc.tensor.transpose(live["eps"][:, i * P : (i + 1) * P], ext[:, i : i + 1].to_broadcast([P, P]), ident[:])
+
+        def se3():
             nc.vector.tensor_reduce(
-                out=gext[:], in_=pe_[:, 0 : 2 * P].rearrange("p (e q) -> p e q", e=2), axis=AX.X, op=ALU.max
+                out=gext[:], in_=live["eps"][:, 0 : 2 * P].rearrange("p (e q) -> p e q", e=2), axis=AX.X, op=ALU.max
             )
             nc.vector.tensor_scalar(
                 out=nmul[:], in0=gext[:, 0:1], scalar1=gext[:, 1:2], scalar2=7.5, op0=ALU.add, op1=ALU.mult
@@ -247,15 +255,13 @@ def tile_splitnn_pa_kernel(tc, x1, x2, W1, b1, W2, b2, noise_std, rr_uniform, ou
                 nc.vector.tensor_tensor(out=nk[:, t, :], in0=noise[:, t, :], in1=keepb[:], op=ALU.mult)
 
         def stt(t):
-            cs = work.tile([P, H], F32, name="cs", tag="cs", bufs=CS_BUFS)
-            live["cs", t] = cs
             nc.vector.scalar_tensor_tensor(
-                out=cs[:], in0=nk[:, t, :], scalar=nmul[:, 0:1], in1=live["bt", 0, t, True][:], op0=ALU.mult, op1=ALU.add
+                out=cs[t][:], in0=nk[:, t, :], scalar=nmul[:, 0:1], in1=live["bt", 0, t, True][:], op0=ALU.mult, op1=ALU.add
             )
 
         def fmin(t):
             nc.vector.tensor_tensor(
-                out=outs[t // 2][:, (t % 2) * H : (t % 2 + 1) * H], in0=live["cs", t][:], in1=live["bt", 1, t, False][:], op=ALU.min
+                out=outs[t // 2][:, (t % 2) * H : (t % 2 + 1) * H], in0=cs[t][:], in1=live["bt", 1, t, False][:], op=ALU.min
             )
 
         def amax(k, j, a, b):
@@ -266,198 +272,206 @@ def tile_splitnn_pa_kernel(tc, x1, x2, W1, b1, W2, b2, noise_std, rr_uniform, ou
         def store0(j):
             nc.sync.dma_start(out=out0_v[:, 2 * j : 2 * j + 2, :], in_=outs[j][:, 0 : 2 * H].rearrange("p (t h) -> p t h", t=2))
 
-        def scale():
+        def sc1():
             nc.vector.tensor_reduce(
                 out=am[:, 0:1], in_=outs[NJ - 1][:, H : 2 * H + PADS], axis=AX.X, op=ALU.max, apply_absolute_value=True
             )
-            pa_ = bank("bt", 3)
-            nc.tensor.transpose(pa_[:, 0:P], am[:, 0:1].to_broadcast([P, P]), ident[:])
+
+        def sc2():
+            live["aps"] = bank()
+            nc.tensor.transpose(live["aps"][:, 0:P], am[:, 0:1].to_broadcast([P, P]), ident[:])
+
+        def sc3():
             nc.vector.tensor_scalar(
-                out=junk_s[:], in0=pa_[:, 0:P], scalar1=1.0 / 448.0, scalar2=None, op0=ALU.mult, op1=ALU.max, accum_out=am[:, 1:2]
+                out=junk_s[:], in0=live["aps"][:, 0:P], scalar1=1.0 / 448.0, scalar2=None, op0=ALU.mult, op1=ALU.max, accum_out=am[:, 1:2]
             )
             nc.vector.reciprocal(out=am[:, 2:3], in_=am[:, 1:2])
 
-        def assist(t):
-            sn = work.tile([P, H], F32, name="sn", tag="sn", bufs=2)
-            sa = work.tile([P, H], F32, name="sa", tag="sa", bufs=2)
-            cs = work.tile([P, H], F32, name="cs", tag="cs", bufs=CS_BUFS)
-            live["cs", t] = cs
-            nc.scalar.activation(out=sn[:], in_=nk[:, t, :], func=ACT.Identity, scale=nmul[:, 0:1])
-            nc.scalar.copy(out=sa[:], in_=live["bt", 0, t, True][:])
-            nc.gpsimd.tensor_tensor(out=cs[:], in0=sn[:], in1=sa[:], op=ALU.add)
-
-        def cast_v(dst, src):
-            nc.vector.tensor_scalar(out=dst, in0=src, scalar1=am[:, 2:3], scalar2=None, op0=ALU.mult, saturate=False)
-
-        def cast_s(dst, src):
-            nc.scalar.activation(out=dst, in_=src, func=ACT.Identity, scale=am[:, 2:3], bias=zero[:, 0:1], saturate=False)
+        def cast(j, a, b, e):
+            if e == "s":
+                nc.scalar.activation(
+                    out=o8[j][:, a:b], in_=outs[j][:, a:b], func=ACT.Identity, scale=am[:, 2:3], bias=zero[:, 0:1], saturate=False
+                )
+            else:
+                nc.vector.tensor_scalar(
+                    out=o8[j][:, a:b], in0=outs[j][:, a:b], scalar1=am[:, 2:3], scalar2=None, op0=ALU.mult, saturate=False
+                )
 
         def store8(j):
             nc.sync.dma_start(out=out1_v[:, 2 * j : 2 * j + 2, :], in_=o8[j][:].bitcast(U8).rearrange("p (t h) -> p t h", t=2))
 
-        vec_a()
-        vec_b()
-        xt(0, 0)
-        wi(0, 0, (("v", 0, 512),))
+        wi(0, 1, "s", 0, 192)
+        va1()
+        va2()
+        va3()
+        wi(0, 1, "v", 192, 512)
+        wi(0, 0, "v", 0, 512)
         wq(0, 0)
-        xt(0, 1)
-        wi(0, 1, (("s", 0, 192), ("v", 192, 512)))
         wq(0, 1)
-        xe(0, 0, "s")
+        va4()
+        vb1()
+        xt(0, 0)
+        xt(0, 1)
         xt(0, 2)
-        xe(0, 1, "s")
         xt(0, 3)
-        xe(0, 2, "v")
+        xt(0, 4)
         xt(0, 5)
+        xt(0, 6)
+        vb2()
+        xe(0, 0, "s")
+        xe(0, 1, "s")
+        xe(0, 2, "s")
         xe(0, 3, "s")
+        xe(0, 4, "s")
+        xe(0, 5, "s")
+        xe(0, 6, "s")
         xq(0, 0)
         xq(0, 1)
-        xt(0, 4)
-        xe(0, 4, "s")
-        mask_noise(0, "g")
-        xt(0, 6)
-        mm(0, (0, 1), 3)
-        xe(0, 5, "v")
+        xq(0, 2)
+        wi(1, 0, "v", 0, 512)
         mm(0, (0, 1), 0)
         mm(0, (0, 1), 1)
         mm(0, (0, 1), 2)
-        ev(0, (0, 1), 3, "s")
+        mm(0, (0, 1), 3)
         xt(0, 7)
-        ev(0, (0, 1), 1, "s")
-        xq(0, 2)
-        ev(0, (0, 1), 0, "v")
-        xe(0, 6, "s")
-        xe(0, 7, "s")
-        ev(0, (0, 1), 2, "v")
-        wi(1, 0, (("v", 0, 512),))
         mm(0, (2,), 1)
         mm(0, (2,), 2)
-        xq(0, 3)
-        bt(0, 0, False)
-        ev(0, (2,), 1, "s")
-        bt(0, 1, False)
-        absum(0)
-        bt(0, 2, False)
-        absum(2)
-        absum(1)
-        mm(0, (2,), 0)
-        bt(0, 3, False)
-        ev(0, (2,), 2, "v")
         mm(0, (2,), 3)
-        mm(0, (3,), 1)
-        ev(0, (2,), 3, "v")
-        ev(0, (3,), 1, "v")
-        mm(0, (3,), 3)
-        ev(0, (2,), 0, "s")
-        mask_noise(7, "g")
-        mm(0, (3,), 0)
-        mm(0, (3,), 2)
-        bt(0, 4, False)
-        absum(3)
-        ev(0, (3,), 3, "s")
-        ev(0, (3,), 0, "v")
-        bt(0, 5, False)
-        mask_noise(2, "g")
-        bt(0, 2, True)
-        absum(4)
-        ev(0, (3,), 2, "v")
-        mask_noise(6, "g")
-        bt(0, 6, False)
+        ev(0, (0, 1), 0, "s")
+        ev(0, (0, 1), 1, "s")
+        ev(0, (0, 1), 2, "s")
+        ev(0, (2,), 2, "s")
+        ev(0, (2,), 3, "s")
+        ev(0, (0, 1), 3, "v")
+        xe(0, 7, "v")
+        xq(0, 3)
         wq(1, 0)
-        absum(5)
-        xt(1, 1)
+        mask_noise(3, "v")
+        mask_noise(0, "v")
+        bt(0, 1, False)
+        bt(0, 2, False)
+        bt(0, 3, False)
+        bt(0, 0, False)
+        mm(0, (2,), 0)
+        mm(0, (3,), 0)
+        mm(0, (3,), 1)
+        mm(0, (3,), 2)
+        mm(0, (3,), 3)
+        absum(1)
+        absum(2)
+        absum(3)
+        ev(0, (3,), 0, "s")
+        absum(0)
+        ev(0, (2,), 0, "v")
+        ev(0, (2,), 1, "v")
+        ev(0, (3,), 1, "v")
+        ev(0, (3,), 2, "v")
+        ev(0, (3,), 3, "v")
+        mask_noise(6, "v")
+        mask_noise(7, "v")
+        mask_noise(4, "v")
+        wi(1, 1, "v", 0, 512)
+        mask_noise(1, "v")
+        mask_noise(2, "v")
+        bt(0, 5, False)
+        bt(0, 4, False)
+        bt(0, 6, False)
         bt(0, 7, False)
-        wi(1, 1, (("v", 0, 512),))
         xt(1, 0)
+        xt(1, 1)
         xt(1, 2)
-        bt(0, 0, True)
+        xt(1, 3)
+        bt(0, 6, True)
+        bt(0, 2, True)
+        absum(5)
+        absum(4)
         absum(6)
         absum(7)
         xe(1, 0, "s")
         xe(1, 1, "s")
-        bt(0, 6, True)
-        wq(1, 1)
-        mask_noise(1, "g")
-        sens_a()
-        mask_noise(3, "g")
-        xt(1, 3)
         xe(1, 2, "s")
-        bt(0, 3, True)
-        xq(1, 0)
         xe(1, 3, "s")
-        xq(1, 1)
-        xt(1, 4)
-        xe(1, 4, "s")
-        bt(0, 7, True)
-        bt(0, 1, True)
-        stt(2)
-        xt(1, 5)
-        stt(1)
-        stt(7)
-        mm(1, (0, 1), 0)
-        xe(1, 5, "s")
-        mask_noise(5, "g")
-        stt(6)
-        ev(1, (0, 1), 0, "s")
-        bt(0, 5, True)
-        xq(1, 2)
-        mm(1, (0, 1), 1)
+        se1()
+        wq(1, 1)
+        se2()
+        bt(0, 3, True)
         bt(0, 4, True)
-        mm(1, (0, 1), 2)
-        ev(1, (0, 1), 1, "s")
-        mask_noise(4, "g")
+        bt(0, 5, True)
+        bt(0, 7, True)
+        xt(1, 7)
+        xt(1, 4)
+        xt(1, 5)
+        xe(1, 4, "s")
+        xe(1, 5, "s")
+        xe(1, 7, "s")
+        se3()
+        xq(1, 0)
+        xq(1, 1)
+        stt(2)
         stt(3)
+        stt(4)
+        stt(6)
+        stt(7)
+        mask_noise(5, "v")
+        mm(1, (0, 1), 0)
+        mm(1, (0, 1), 1)
+        bt(0, 0, True)
+        bt(0, 1, True)
+        mm(1, (0, 1), 2)
         mm(1, (0, 1), 3)
+        xt(1, 6)
+        ev(1, (0, 1), 0, "s")
+        ev(1, (0, 1), 1, "s")
         ev(1, (0, 1), 2, "s")
         ev(1, (0, 1), 3, "s")
-        xt(1, 6)
-        xt(1, 7)
-        stt(0)
         xe(1, 6, "s")
-        bt(1, 0, False)
-        xe(1, 7, "s")
+        stt(0)
+        stt(1)
         stt(5)
-        stt(4)
-        bt(1, 2, False)
-        fmin(0)
+        xq(1, 2)
         xq(1, 3)
-        bt(1, 3, False)
+        bt(1, 0, False)
         bt(1, 1, False)
-        fmin(1)
+        bt(1, 2, False)
+        bt(1, 3, False)
         mm(1, (2, 3), 0)
         mm(1, (2, 3), 1)
-        fmin(3)
-        fmin(2)
-        ev(1, (2, 3), 0, "s")
-        ev(1, (2, 3), 1, "s")
         mm(1, (2, 3), 2)
         mm(1, (2, 3), 3)
+        ev(1, (2, 3), 0, "s")
+        ev(1, (2, 3), 1, "s")
         ev(1, (2, 3), 2, "s")
-        amax(0, 0, 0, 2 * H)
         ev(1, (2, 3), 3, "s")
-        bt(1, 4, False)
+        fmin(0)
+        fmin(1)
+        fmin(2)
+        fmin(3)
+        amax(0, 0, 0, 2 * H)
         amax(1, 1, 0, 2 * H)
+        store0(0)
         store0(1)
+        bt(1, 4, False)
         bt(1, 5, False)
         bt(1, 6, False)
-        fmin(4)
         bt(1, 7, False)
-        store0(0)
+        fmin(4)
         fmin(5)
-        fmin(7)
-        store0(2)
         fmin(6)
-        amax(2, 2, 0, 2 * H)
-        store0(3)
+        fmin(7)
         amax(3, 3, 0, H)
-        scale()
-        cast_v(o8[0][:], outs[0][:])
-        cast_s(o8[2][:, H : 2 * H], outs[2][:, H : 2 * H])
-        cast_s(o8[2][:, 0:H], outs[2][:, 0:H])
+        amax(2, 2, 0, 2 * H)
+        sc1()
+        store0(2)
+        store0(3)
+        sc2()
+        sc3()
+        cast(0, 0, 2 * H, "v")
+        cast(1, 0, 2 * H, "v")
+        cast(3, 0, H, "v")
         store8(0)
-        cast_s(o8[3][:, H : 2 * H], outs[3][:, H : 2 * H])
-        store8(2)
-        cast_v(o8[1][:], outs[1][:])
-        cast_v(o8[3][:, 0:H], outs[3][:, 0:H])
         store8(1)
+        cast(2, 0, H, "s")
+        cast(2, H, 2 * H, "s")
+        cast(3, H, 2 * H, "s")
+        store8(2)
         store8(3)

@@ -304,10 +304,8 @@ def tile_splitnn_pa_kernel(tc, x1, x2, W1, b1, W2, b2, noise_std, rr_uniform, ou
         va1()
         va2()
         va3()
-        wi(0, 1, "v", 192, 512)
         wi(0, 0, "v", 0, 512)
-        wq(0, 0)
-        wq(0, 1)
+        wi(0, 1, "v", 192, 512)
         va4()
         vb1()
         xt(0, 0)
@@ -318,41 +316,44 @@ def tile_splitnn_pa_kernel(tc, x1, x2, W1, b1, W2, b2, noise_std, rr_uniform, ou
         xt(0, 5)
         xt(0, 6)
         vb2()
-        xe(0, 0, "s")
         xe(0, 1, "s")
         xe(0, 2, "s")
         xe(0, 3, "s")
         xe(0, 4, "s")
         xe(0, 5, "s")
         xe(0, 6, "s")
+        xe(0, 0, "v")
+        wq(0, 0)
+        wq(0, 1)
         xq(0, 0)
         xq(0, 1)
-        xq(0, 2)
         wi(1, 0, "v", 0, 512)
+        xq(0, 2)
+        wq(1, 0)
         mm(0, (0, 1), 0)
         mm(0, (0, 1), 1)
         mm(0, (0, 1), 2)
         mm(0, (0, 1), 3)
         xt(0, 7)
-        mm(0, (2,), 1)
         mm(0, (2,), 2)
         mm(0, (2,), 3)
         ev(0, (0, 1), 0, "s")
         ev(0, (0, 1), 1, "s")
         ev(0, (0, 1), 2, "s")
+        ev(0, (0, 1), 3, "s")
         ev(0, (2,), 2, "s")
         ev(0, (2,), 3, "s")
-        ev(0, (0, 1), 3, "v")
         xe(0, 7, "v")
         xq(0, 3)
-        wq(1, 0)
-        mask_noise(3, "v")
         mask_noise(0, "v")
+        mask_noise(3, "v")
+        mask_noise(1, "v")
         bt(0, 1, False)
         bt(0, 2, False)
         bt(0, 3, False)
         bt(0, 0, False)
         mm(0, (2,), 0)
+        mm(0, (2,), 1)
         mm(0, (3,), 0)
         mm(0, (3,), 1)
         mm(0, (3,), 2)
@@ -360,19 +361,19 @@ def tile_splitnn_pa_kernel(tc, x1, x2, W1, b1, W2, b2, noise_std, rr_uniform, ou
         absum(1)
         absum(2)
         absum(3)
-        ev(0, (3,), 0, "s")
         absum(0)
+        ev(0, (3,), 0, "s")
+        ev(0, (3,), 3, "s")
         ev(0, (2,), 0, "v")
         ev(0, (2,), 1, "v")
         ev(0, (3,), 1, "v")
         ev(0, (3,), 2, "v")
-        ev(0, (3,), 3, "v")
+        mask_noise(2, "v")
         mask_noise(6, "v")
         mask_noise(7, "v")
-        mask_noise(4, "v")
         wi(1, 1, "v", 0, 512)
-        mask_noise(1, "v")
-        mask_noise(2, "v")
+        mask_noise(4, "v")
+        mask_noise(5, "v")
         bt(0, 5, False)
         bt(0, 4, False)
         bt(0, 6, False)
@@ -380,9 +381,9 @@ def tile_splitnn_pa_kernel(tc, x1, x2, W1, b1, W2, b2, noise_std, rr_uniform, ou
         xt(1, 0)
         xt(1, 1)
         xt(1, 2)
-        xt(1, 3)
         bt(0, 6, True)
-        bt(0, 2, True)
+        bt(0, 7, True)
+        xt(1, 3)
         absum(5)
         absum(4)
         absum(6)
@@ -394,41 +395,40 @@ def tile_splitnn_pa_kernel(tc, x1, x2, W1, b1, W2, b2, noise_std, rr_uniform, ou
         se1()
         wq(1, 1)
         se2()
+        bt(0, 2, True)
+        xt(1, 4)
+        xt(1, 5)
+        xt(1, 7)
         bt(0, 3, True)
         bt(0, 4, True)
         bt(0, 5, True)
-        bt(0, 7, True)
-        xt(1, 7)
-        xt(1, 4)
-        xt(1, 5)
         xe(1, 4, "s")
         xe(1, 5, "s")
         xe(1, 7, "s")
         se3()
         xq(1, 0)
         xq(1, 1)
+        stt(6)
+        stt(7)
         stt(2)
         stt(3)
         stt(4)
-        stt(6)
-        stt(7)
-        mask_noise(5, "v")
+        stt(5)
+        xq(1, 2)
         mm(1, (0, 1), 0)
         mm(1, (0, 1), 1)
-        bt(0, 0, True)
-        bt(0, 1, True)
         mm(1, (0, 1), 2)
         mm(1, (0, 1), 3)
+        bt(0, 1, True)
         xt(1, 6)
+        bt(0, 0, True)
         ev(1, (0, 1), 0, "s")
         ev(1, (0, 1), 1, "s")
         ev(1, (0, 1), 2, "s")
         ev(1, (0, 1), 3, "s")
         xe(1, 6, "s")
-        stt(0)
         stt(1)
-        stt(5)
-        xq(1, 2)
+        stt(0)
         xq(1, 3)
         bt(1, 0, False)
         bt(1, 1, False)
@@ -458,8 +458,8 @@ def tile_splitnn_pa_kernel(tc, x1, x2, W1, b1, W2, b2, noise_std, rr_uniform, ou
         fmin(5)
         fmin(6)
         fmin(7)
-        amax(3, 3, 0, H)
         amax(2, 2, 0, 2 * H)
+        amax(3, 3, 0, H)
         sc1()
         store0(2)
         store0(3)

@@ -15,12 +15,19 @@ AX = mybir.AxisListType
 
 P = 128
 B, F, H = 1024, 1024, 512
+K_PASS = 4 * P
 NT = B // P
-NG = F // 512
-NC = H // P
 NJ = NT // 2
-FLOPS = 2 * 2 * B * F * H
+NG = F // K_PASS
+NH = H // P
+PAIR = 2 * P
+BANK = 512
 PADS = 8
+P_KEEP = 0.95
+INV_EPS = 7.5
+FP8_MAX = 448.0
+W_SPLIT = 192
+FLOPS = 2 * 2 * B * F * H
 
 
 def tile_splitnn_pa_kernel(tc, x1, x2, W1, b1, W2, b2, noise_std, rr_uniform, out_0, out_1):
@@ -34,7 +41,7 @@ def tile_splitnn_pa_kernel(tc, x1, x2, W1, b1, W2, b2, noise_std, rr_uniform, ou
         ctx.enter_context(tc.manual_schedule())
 
         def bank():
-            t = psum.tile([P, 512], F32, name="ps", tag="ps", bufs=8)
+            t = psum.tile([P, BANK], F32, name="ps", tag="ps", bufs=8)
             return t
 
         ident = keep.tile([P, P], F32, name="ident")
@@ -42,15 +49,15 @@ def tile_splitnn_pa_kernel(tc, x1, x2, W1, b1, W2, b2, noise_std, rr_uniform, ou
         warm = keep.tile([P, 1], F32, name="warm")
         vrow = keep.tile([P, P], BF16, name="vrow")
         vrow32 = keep.tile([P, P], F32, name="vrow32")
-        vcol = keep.tile([P, 12], F32, name="vcol")
-        kcol = keep.tile([P, NC], F32, name="kcol")
-        identk = keep.tile([P, NC, P], F32, name="identk")
+        vcol = keep.tile([P, 3 * NH], F32, name="vcol")
+        kcol = keep.tile([P, NH], F32, name="kcol")
+        identk = keep.tile([P, NH, P], F32, name="identk")
         keepb = keep.tile([P, H], BF16, name="keepb")
         noise = keep.tile([P, NT, H], BF16, name="noise")
         nk = keep.tile([P, NT, H], BF16, name="nk")
         norms = keep.tile([P, NT], F32, name="norms")
         junk_n = keep.tile([P, NT], F32, name="junkn")
-        junk_s = keep.tile([P, P], F32, name="junks")
+        junk_s = keep.tile([P, 2 * P], F32, name="junks")
         ext = keep.tile([P, 2], F32, name="ext")
         gext = keep.tile([P, 2], F32, name="gext")
         nmul = keep.tile([P, 1], F32, name="nmul")
@@ -67,15 +74,15 @@ def tile_splitnn_pa_kernel(tc, x1, x2, W1, b1, W2, b2, noise_std, rr_uniform, ou
         for c in range(2):
             wcodes[c] = keep.tile([P, NG, H], U32, name="wcodes%d" % c, align_bytes=64)
             wscales[c] = keep.tile([P, NG, H], U8, name="wscales%d" % c, align_bytes=64)
-            res_t[c] = keep.tile([P, NC, B], F32, name="rest%d" % c)
+            res_t[c] = keep.tile([P, NH, B], F32, name="rest%d" % c)
             for g in range(NG):
                 wraw[c][g] = keep.tile([P, 4, H], BF16, name="wraw%d%d" % (c, g))
                 wgrp[c][g] = keep.tile([P, H, 4], BF16, name="wgrp%d%d" % (c, g), align_bytes=64)
             for j in range(NJ):
                 xraw[c][j] = keep.tile([P, 2, F], BF16, name="xraw%d%d" % (c, j))
-                xgrp[c][j] = keep.tile([P, NG, 2 * P, 4], BF16, name="xgrp%d%d" % (c, j), align_bytes=64)
-                xcodes[c][j] = keep.tile([P, NG, 2 * P], U32, name="xcodes%d%d" % (c, j), align_bytes=64)
-                xscales[c][j] = keep.tile([P, NG, 2 * P], U8, name="xscales%d%d" % (c, j), align_bytes=64)
+                xgrp[c][j] = keep.tile([P, NG, PAIR, 4], BF16, name="xgrp%d%d" % (c, j), align_bytes=64)
+                xcodes[c][j] = keep.tile([P, NG, PAIR], U32, name="xcodes%d%d" % (c, j), align_bytes=64)
+                xscales[c][j] = keep.tile([P, NG, PAIR], U8, name="xscales%d%d" % (c, j), align_bytes=64)
         junk = [None] * 2
         for i in range(2):
             junk[i] = keep.tile([P, H], BF16, name="junk%d" % i)
@@ -87,23 +94,23 @@ def tile_splitnn_pa_kernel(tc, x1, x2, W1, b1, W2, b2, noise_std, rr_uniform, ou
         for j in range(NJ):
             outs[j] = keep.tile([P, 2 * H + (PADS if j == NJ - 1 else 0)], F32, name="outs%d" % j)
             o8[j] = keep.tile([P, 2 * H], FP8, name="o8%d" % j)
+        pads = outs[NJ - 1][:, 2 * H : 2 * H + PADS]
         out0_v = out_0.rearrange("(p t) h -> p t h", t=NT)
         out1_v = out_1.rearrange("(p t) h -> p t h", t=NT)
         noise_v = noise_std.rearrange("(p t) h -> p t h", t=NT)
-        live = {}
+        ps = {}
 
         make_identity(nc, ident[:])
         nc.vector.memset(zero[:], 0.0)
         nc.scalar.activation(out=warm[:], in_=zero[:], func=ACT.Abs)
         nc.vector.memset(vrow[:], 0.0)
-        nc.vector.memset(outs[NJ - 1][:, 2 * H : 2 * H + PADS], 0.0)
-        nc.sync.dma_start(out=vrow[0:4, :], in_=b1.rearrange("(c p) -> c p", p=P))
-        nc.sync.dma_start(out=vrow[4:8, :], in_=b2.rearrange("(c p) -> c p", p=P))
-        nc.sync.dma_start(out=vrow[8:12, :], in_=rr_uniform.rearrange("(c p) -> c p", p=P))
+        nc.vector.memset(pads, 0.0)
+        for i, vec in enumerate((b1, b2, rr_uniform)):
+            nc.sync.dma_start(out=vrow[NH * i : NH * (i + 1), :], in_=vec.rearrange("(h p) -> h p", p=P))
 
         def load_w(c, g):
             nc.sync.dma_start(
-                out=wraw[c][g][:], in_=ws_in[c][g * 512 : (g + 1) * 512, :].rearrange("(p j) w -> p j w", j=4)
+                out=wraw[c][g][:], in_=ws_in[c][g * K_PASS : (g + 1) * K_PASS, :].rearrange("(p e) w -> p e w", e=4)
             )
 
         def load_x(c, j):
@@ -111,94 +118,90 @@ def tile_splitnn_pa_kernel(tc, x1, x2, W1, b1, W2, b2, noise_std, rr_uniform, ou
                 out=xraw[c][j][:], in_=xs_in[c].rearrange("(p t) k -> p t k", t=NT)[:, 2 * j : 2 * j + 2, :]
             )
 
-        def load_n(i):
+        def load_noise(i):
             nc.sync.dma_start(out=noise[:, 4 * i : 4 * i + 4, :], in_=noise_v[:, 4 * i : 4 * i + 4, :])
 
-        load_w(0, 0)
-        load_w(0, 1)
-        load_x(0, 0)
-        load_x(0, 1)
-        load_x(0, 2)
-        load_x(0, 3)
-        load_w(1, 0)
-        load_w(1, 1)
-        load_x(1, 0)
-        load_x(1, 1)
-        load_n(0)
-        load_x(1, 2)
-        load_x(1, 3)
-        load_n(1)
+        for g in range(NG):
+            load_w(0, g)
+        for j in range(NJ):
+            load_x(0, j)
+        for g in range(NG):
+            load_w(1, g)
+        for i in range(2):
+            load_x(1, 2 * i)
+            load_x(1, 2 * i + 1)
+            load_noise(i)
 
-        def va1():
+        def widen_vectors():
             nc.vector.tensor_copy(out=vrow32[:], in_=vrow[:])
 
-        def va2():
-            live["vps"] = bank()
-            nc.tensor.transpose(live["vps"][:, 0:P], vrow32[:], ident[:])
+        def turn_vectors():
+            ps["vec"] = bank()
+            nc.tensor.transpose(ps["vec"][:, 0:P], vrow32[:], ident[:])
 
-        def va3():
-            nc.vector.tensor_copy(out=vcol[:], in_=live["vps"][:, 0:12])
-            nc.vector.tensor_scalar(out=kcol[:], in0=vcol[:, 8:12], scalar1=0.95, scalar2=None, op0=ALU.is_lt)
+        def take_vectors():
+            nc.vector.tensor_copy(out=vcol[:], in_=ps["vec"][:, 0 : 3 * NH])
+            nc.vector.tensor_scalar(out=kcol[:], in0=vcol[:, 2 * NH : 3 * NH], scalar1=P_KEEP, scalar2=None, op0=ALU.is_lt)
 
-        def va4():
-            for h in range(NC):
+        def mask_identities():
+            for h in range(NH):
                 nc.gpsimd.tensor_scalar(
                     out=identk[:, h, :], in0=ident[:], scalar1=kcol[:, h : h + 1], scalar2=0.0, op0=ALU.mult, op1=ALU.add
                 )
 
-        def vb1():
-            live["kps"] = bank()
-            for h in range(NC):
-                nc.tensor.transpose(live["kps"][:, h * P : (h + 1) * P], kcol[:, h : h + 1].to_broadcast([P, P]), ident[:])
+        def spread_keep():
+            ps["keep"] = bank()
+            for h in range(NH):
+                nc.tensor.transpose(ps["keep"][:, h * P : (h + 1) * P], kcol[:, h : h + 1].to_broadcast([P, P]), ident[:])
 
-        def vb2():
-            nc.scalar.copy(out=keepb[:], in_=live["kps"][:])
+        def take_keep():
+            nc.scalar.copy(out=keepb[:], in_=ps["keep"][:])
 
-        def wi(c, g, e, a, b):
-            src = wraw[c][g][:, :, a:b].rearrange("p j w -> p w j")
-            if e == "s":
-                nc.scalar.copy(out=wgrp[c][g][:, a:b, :], in_=src)
+        def interleave_w(c, g, engine, lo, hi):
+            src = wraw[c][g][:, :, lo:hi].rearrange("p e w -> p w e")
+            if engine == "s":
+                nc.scalar.copy(out=wgrp[c][g][:, lo:hi, :], in_=src)
             else:
-                nc.vector.tensor_copy(out=wgrp[c][g][:, a:b, :], in_=src)
+                nc.vector.tensor_copy(out=wgrp[c][g][:, lo:hi, :], in_=src)
 
-        def wq(c, g):
+        def quantize_w(c, g):
             nc.vector.quantize_mx(
                 out=wcodes[c][:, g, :].bitcast(FP8X4),
                 scales=wscales[c][:, g, :],
-                in_=wgrp[c][g][:].rearrange("p w j -> p (w j)"),
+                in_=wgrp[c][g][:].rearrange("p w e -> p (w e)"),
             )
 
-        def xt(c, t):
+        def turn_x(c, t):
             words = xraw[c][t // 2][:, t % 2, :].bitcast(F32)
             pt = psum.tile([P, 2 * NG, P], F32, name="ps", tag="ps", bufs=8)
-            live["xt", c, t] = pt
+            ps["x", c, t] = pt
             for g in range(NG):
                 for u in range(2):
                     nc.tensor.transpose(pt[:, 2 * g + u, :], words[:, 256 * g + u : 256 * (g + 1) : 2], ident[:])
 
-        def xe(c, t, e):
+        def take_x(c, t, engine):
             i = t % 2
             dst = xgrp[c][t // 2][:].bitcast(F32)[:, :, i * P : (i + 1) * P, :]
-            src = live["xt", c, t][:].rearrange("p (g u) r -> p g r u", g=NG)
-            if e == "s":
+            src = ps["x", c, t][:].rearrange("p (g u) r -> p g r u", g=NG)
+            if engine == "s":
                 nc.scalar.copy(out=dst, in_=src)
             else:
                 nc.vector.tensor_copy(out=dst, in_=src)
 
-        def xq(c, j):
+        def quantize_x(c, j):
             nc.vector.quantize_mx(
                 out=xcodes[c][j][:].rearrange("p g r -> p (g r)").bitcast(FP8X4),
                 scales=xscales[c][j][:].rearrange("p g r -> p (g r)"),
-                in_=xgrp[c][j][:].rearrange("p g r j -> p (g r j)"),
+                in_=xgrp[c][j][:].rearrange("p g r e -> p (g r e)"),
             )
 
-        def mm(c, js, h):
+        def project(c, pairs, h):
             acc = bank()
-            live["acc", c, js[0], h] = acc
-            for i, j in enumerate(js):
+            ps["acc", c, pairs[0], h] = acc
+            for i, j in enumerate(pairs):
                 for g in range(NG):
                     nc.tensor.matmul_mx(
-                        out=acc[:, i * 256 : (i + 1) * 256],
+                        out=acc[:, i * PAIR : (i + 1) * PAIR],
                         lhsT=wcodes[c][:, g, h * P : (h + 1) * P].bitcast(FP8X4),
                         lhsT_scale=wscales[c][:, g, h * P : (h + 1) * P],
                         rhs=xcodes[c][j][:, g, :].bitcast(FP8X4),
@@ -207,271 +210,222 @@ def tile_splitnn_pa_kernel(tc, x1, x2, W1, b1, W2, b2, noise_std, rr_uniform, ou
                         stop=(g == NG - 1),
                     )
 
-        def ev(c, js, h, e):
-            src = live["acc", c, js[0], h][:, 0 : 256 * len(js)]
-            dst = res_t[c][:, h, 256 * js[0] : 256 * (js[0] + len(js))]
-            bias = vcol[:, 4 * c + h : 4 * c + h + 1]
-            if e == "s":
+        def add_bias(c, pairs, h, engine):
+            src = ps["acc", c, pairs[0], h][:, 0 : PAIR * len(pairs)]
+            dst = res_t[c][:, h, PAIR * pairs[0] : PAIR * (pairs[0] + len(pairs))]
+            bias = vcol[:, NH * c + h : NH * c + h + 1]
+            if engine == "s":
                 nc.scalar.activation(out=dst, in_=src, func=ACT.Identity, bias=bias, scale=1.0)
             else:
                 nc.vector.tensor_scalar(out=dst, in0=src, scalar1=bias, scalar2=None, op0=ALU.add)
 
-        def bt(c, t, masked):
+        def turn_back(c, t, masked):
             pb = bank()
-            live["bt", c, t, masked] = pb
-            for h in range(NC):
+            ps["back", c, t, masked] = pb
+            for h in range(NH):
                 nc.tensor.transpose(
                     pb[:, h * P : (h + 1) * P], res_t[c][:, h, t * P : (t + 1) * P], identk[:, h, :] if masked else ident[:]
                 )
 
-        def absum(t):
+        def row_norm(t):
             nc.scalar.activation(
-                out=junk[t % 2][:], in_=live["bt", 0, t, False][:], func=ACT.Abs, accum_out=norms[:, t : t + 1]
+                out=junk[t % 2][:], in_=ps["back", 0, t, False][:], func=ACT.Abs, accum_out=norms[:, t : t + 1]
             )
 
-        def se1():
+        def norm_extremes():
             nc.vector.tensor_reduce(out=ext[:, 0:1], in_=norms[:], axis=AX.X, op=ALU.max)
             nc.vector.tensor_scalar(
                 out=junk_n[:], in0=norms[:], scalar1=-1.0, scalar2=None, op0=ALU.mult, op1=ALU.max, accum_out=ext[:, 1:2]
             )
 
-        def se2():
-            live["eps"] = bank()
+        def spread_extremes():
+            ps["ext"] = bank()
             for i in range(2):
-                nc.tensor.transpose(live["eps"][:, i * P : (i + 1) * P], ext[:, i : i + 1].to_broadcast([P, P]), ident[:])
+                nc.tensor.transpose(ps["ext"][:, i * P : (i + 1) * P], ext[:, i : i + 1].to_broadcast([P, P]), ident[:])
 
-        def se3():
+        def noise_factor():
             nc.vector.tensor_reduce(
-                out=gext[:], in_=live["eps"][:, 0 : 2 * P].rearrange("p (e q) -> p e q", e=2), axis=AX.X, op=ALU.max
+                out=gext[:], in_=ps["ext"][:, 0 : 2 * P].rearrange("p (i q) -> p i q", i=2), axis=AX.X, op=ALU.max
             )
             nc.vector.tensor_scalar(
-                out=nmul[:], in0=gext[:, 0:1], scalar1=gext[:, 1:2], scalar2=7.5, op0=ALU.add, op1=ALU.mult
+                out=nmul[:], in0=gext[:, 0:1], scalar1=gext[:, 1:2], scalar2=INV_EPS, op0=ALU.add, op1=ALU.mult
             )
 
-        def mask_noise(t, e):
-            if e == "g":
-                nc.gpsimd.tensor_tensor(out=nk[:, t, :], in0=noise[:, t, :], in1=keepb[:], op=ALU.mult)
-            else:
-                nc.vector.tensor_tensor(out=nk[:, t, :], in0=noise[:, t, :], in1=keepb[:], op=ALU.mult)
-
-        def stt(t):
-            nc.vector.scalar_tensor_tensor(
-                out=cs[t][:], in0=nk[:, t, :], scalar=nmul[:, 0:1], in1=live["bt", 0, t, True][:], op0=ALU.mult, op1=ALU.add
-            )
-
-        def fmin(t):
+        def mask_noise(i):
             nc.vector.tensor_tensor(
-                out=outs[t // 2][:, (t % 2) * H : (t % 2 + 1) * H], in0=cs[t][:], in1=live["bt", 1, t, False][:], op=ALU.min
+                out=nk[:, 4 * i : 4 * i + 4, :],
+                in0=noise[:, 4 * i : 4 * i + 4, :],
+                in1=keepb[:].unsqueeze(1).to_broadcast([P, 4, H]),
+                op=ALU.mult,
             )
 
-        def amax(k, j, a, b):
-            nc.vector.tensor_reduce(
-                out=outs[NJ - 1][:, 2 * H + k : 2 * H + k + 1], in_=outs[j][:, a:b], axis=AX.X, op=ALU.max, apply_absolute_value=True
+        def add_noise(t):
+            nc.vector.scalar_tensor_tensor(
+                out=cs[t][:], in0=nk[:, t, :], scalar=nmul[:, 0:1], in1=ps["back", 0, t, True][:], op0=ALU.mult, op1=ALU.add
             )
 
-        def store0(j):
+        def fuse(t):
+            nc.vector.tensor_tensor(
+                out=outs[t // 2][:, (t % 2) * H : (t % 2 + 1) * H], in0=cs[t][:], in1=ps["back", 1, t, False][:], op=ALU.min
+            )
+
+        def partial_amax(dst, j, lo, hi):
+            nc.vector.tensor_reduce(out=dst, in_=outs[j][:, lo:hi], axis=AX.X, op=ALU.max, apply_absolute_value=True)
+
+        def store_out0(j):
             nc.sync.dma_start(out=out0_v[:, 2 * j : 2 * j + 2, :], in_=outs[j][:, 0 : 2 * H].rearrange("p (t h) -> p t h", t=2))
 
-        def sc1():
-            nc.vector.tensor_reduce(
-                out=am[:, 0:1], in_=outs[NJ - 1][:, H : 2 * H + PADS], axis=AX.X, op=ALU.max, apply_absolute_value=True
-            )
+        def spread_amax():
+            ps["amax"] = bank()
+            for i in range(2):
+                nc.tensor.transpose(ps["amax"][:, i * P : (i + 1) * P], am[:, i : i + 1].to_broadcast([P, P]), ident[:])
 
-        def sc2():
-            live["aps"] = bank()
-            nc.tensor.transpose(live["aps"][:, 0:P], am[:, 0:1].to_broadcast([P, P]), ident[:])
-
-        def sc3():
+        def cast_factor():
             nc.vector.tensor_scalar(
-                out=junk_s[:], in0=live["aps"][:, 0:P], scalar1=1.0 / 448.0, scalar2=None, op0=ALU.mult, op1=ALU.max, accum_out=am[:, 1:2]
+                out=junk_s[:], in0=ps["amax"][:, 0 : 2 * P], scalar1=1.0 / FP8_MAX, scalar2=None, op0=ALU.mult, op1=ALU.max,
+                accum_out=am[:, 2:3],
             )
-            nc.vector.reciprocal(out=am[:, 2:3], in_=am[:, 1:2])
+            nc.vector.reciprocal(out=am[:, 3:4], in_=am[:, 2:3])
 
-        def cast(j, a, b, e):
-            if e == "s":
+        def cast(j, lo, hi, engine):
+            if engine == "s":
                 nc.scalar.activation(
-                    out=o8[j][:, a:b], in_=outs[j][:, a:b], func=ACT.Identity, scale=am[:, 2:3], bias=zero[:, 0:1], saturate=False
+                    out=o8[j][:, lo:hi], in_=outs[j][:, lo:hi], func=ACT.Identity, scale=am[:, 3:4], bias=zero[:, 0:1], saturate=False
                 )
             else:
                 nc.vector.tensor_scalar(
-                    out=o8[j][:, a:b], in0=outs[j][:, a:b], scalar1=am[:, 2:3], scalar2=None, op0=ALU.mult, saturate=False
+                    out=o8[j][:, lo:hi], in0=outs[j][:, lo:hi], scalar1=am[:, 3:4], scalar2=None, op0=ALU.mult, saturate=False
                 )
 
-        def store8(j):
+        def store_out1(j):
             nc.sync.dma_start(out=out1_v[:, 2 * j : 2 * j + 2, :], in_=o8[j][:].bitcast(U8).rearrange("p (t h) -> p t h", t=2))
 
-        wi(0, 1, "s", 0, 192)
-        va1()
-        va2()
-        va3()
-        wi(0, 0, "v", 0, 512)
-        wi(0, 1, "v", 192, 512)
-        va4()
-        vb1()
-        xt(0, 0)
-        xt(0, 1)
-        xt(0, 2)
-        xt(0, 3)
-        xt(0, 4)
-        xt(0, 5)
-        xt(0, 6)
-        vb2()
-        xe(0, 1, "s")
-        xe(0, 2, "s")
-        xe(0, 3, "s")
-        xe(0, 4, "s")
-        xe(0, 5, "s")
-        xe(0, 6, "s")
-        xe(0, 0, "v")
-        wq(0, 0)
-        wq(0, 1)
-        xq(0, 0)
-        xq(0, 1)
-        wi(1, 0, "v", 0, 512)
-        xq(0, 2)
-        wq(1, 0)
-        mm(0, (0, 1), 0)
-        mm(0, (0, 1), 1)
-        mm(0, (0, 1), 2)
-        mm(0, (0, 1), 3)
-        xt(0, 7)
-        mm(0, (2,), 2)
-        mm(0, (2,), 3)
-        ev(0, (0, 1), 0, "s")
-        ev(0, (0, 1), 1, "s")
-        ev(0, (0, 1), 2, "s")
-        ev(0, (0, 1), 3, "s")
-        ev(0, (2,), 2, "s")
-        ev(0, (2,), 3, "s")
-        xe(0, 7, "v")
-        xq(0, 3)
-        mask_noise(0, "v")
-        mask_noise(3, "v")
-        mask_noise(1, "v")
-        bt(0, 1, False)
-        bt(0, 2, False)
-        bt(0, 3, False)
-        bt(0, 0, False)
-        mm(0, (2,), 0)
-        mm(0, (2,), 1)
-        mm(0, (3,), 0)
-        mm(0, (3,), 1)
-        mm(0, (3,), 2)
-        mm(0, (3,), 3)
-        absum(1)
-        absum(2)
-        absum(3)
-        absum(0)
-        ev(0, (3,), 0, "s")
-        ev(0, (3,), 3, "s")
-        ev(0, (2,), 0, "v")
-        ev(0, (2,), 1, "v")
-        ev(0, (3,), 1, "v")
-        ev(0, (3,), 2, "v")
-        mask_noise(2, "v")
-        mask_noise(6, "v")
-        mask_noise(7, "v")
-        wi(1, 1, "v", 0, 512)
-        mask_noise(4, "v")
-        mask_noise(5, "v")
-        bt(0, 5, False)
-        bt(0, 4, False)
-        bt(0, 6, False)
-        bt(0, 7, False)
-        xt(1, 0)
-        xt(1, 1)
-        xt(1, 2)
-        bt(0, 6, True)
-        bt(0, 7, True)
-        xt(1, 3)
-        absum(5)
-        absum(4)
-        absum(6)
-        absum(7)
-        xe(1, 0, "s")
-        xe(1, 1, "s")
-        xe(1, 2, "s")
-        xe(1, 3, "s")
-        se1()
-        wq(1, 1)
-        se2()
-        bt(0, 2, True)
-        xt(1, 4)
-        xt(1, 5)
-        xt(1, 7)
-        bt(0, 3, True)
-        bt(0, 4, True)
-        bt(0, 5, True)
-        xe(1, 4, "s")
-        xe(1, 5, "s")
-        xe(1, 7, "s")
-        se3()
-        xq(1, 0)
-        xq(1, 1)
-        stt(6)
-        stt(7)
-        stt(2)
-        stt(3)
-        stt(4)
-        stt(5)
-        xq(1, 2)
-        mm(1, (0, 1), 0)
-        mm(1, (0, 1), 1)
-        mm(1, (0, 1), 2)
-        mm(1, (0, 1), 3)
-        bt(0, 1, True)
-        xt(1, 6)
-        bt(0, 0, True)
-        ev(1, (0, 1), 0, "s")
-        ev(1, (0, 1), 1, "s")
-        ev(1, (0, 1), 2, "s")
-        ev(1, (0, 1), 3, "s")
-        xe(1, 6, "s")
-        stt(1)
-        stt(0)
-        xq(1, 3)
-        bt(1, 0, False)
-        bt(1, 1, False)
-        bt(1, 2, False)
-        bt(1, 3, False)
-        mm(1, (2, 3), 0)
-        mm(1, (2, 3), 1)
-        mm(1, (2, 3), 2)
-        mm(1, (2, 3), 3)
-        ev(1, (2, 3), 0, "s")
-        ev(1, (2, 3), 1, "s")
-        ev(1, (2, 3), 2, "s")
-        ev(1, (2, 3), 3, "s")
-        fmin(0)
-        fmin(1)
-        fmin(2)
-        fmin(3)
-        amax(0, 0, 0, 2 * H)
-        amax(1, 1, 0, 2 * H)
-        store0(0)
-        store0(1)
-        bt(1, 4, False)
-        bt(1, 5, False)
-        bt(1, 6, False)
-        bt(1, 7, False)
-        fmin(4)
-        fmin(5)
-        fmin(6)
-        fmin(7)
-        amax(2, 2, 0, 2 * H)
-        amax(3, 3, 0, H)
-        sc1()
-        store0(2)
-        store0(3)
-        sc2()
-        sc3()
-        cast(0, 0, 2 * H, "v")
-        cast(1, 0, 2 * H, "v")
+
+        interleave_w(0, 1, "s", 0, W_SPLIT)
+        interleave_w(0, 0, "v", 0, H)
+        widen_vectors()
+        turn_vectors()
+        for t in range(4):
+            turn_x(0, t)
+        for t in range(4):
+            take_x(0, t, "s")
+        take_vectors()
+        interleave_w(0, 1, "v", W_SPLIT, H)
+        for g in range(NG):
+            quantize_w(0, g)
+        for j in range(2):
+            quantize_x(0, j)
+        mask_identities()
+
+        spread_keep()
+        for t in range(4, 8):
+            turn_x(0, t)
+        for h in range(NH):
+            project(0, (0, 1), h)
+        turn_x(1, 0)
+        for t in range(4, 8):
+            take_x(0, t, "s")
+        take_keep()
+        for h in range(3):
+            add_bias(0, (0, 1), h, "s")
+        quantize_x(0, 2)
+        interleave_w(1, 0, "v", 0, H)
+        add_bias(0, (0, 1), 3, "v")
+        quantize_x(0, 3)
+        quantize_w(1, 0)
+        mask_noise(0)
+
+        for h in range(2):
+            project(0, (2,), h)
+        for t in range(4):
+            turn_back(0, t, False)
+        for h in range(2, 4):
+            project(0, (2,), h)
+        for h in range(NH):
+            project(0, (3,), h)
+        for h in range(2):
+            add_bias(0, (2,), h, "s")
+        for t in range(4):
+            row_norm(t)
+        add_bias(0, (3,), 0, "s")
+        for h in range(2, 4):
+            add_bias(0, (2,), h, "v")
+        for h in range(1, 4):
+            add_bias(0, (3,), h, "v")
+        interleave_w(1, 1, "v", 0, H)
+        take_x(1, 0, "v")
+        mask_noise(1)
+
+        for t in range(4, 8):
+            turn_back(0, t, False)
+        for t in range(1, 5):
+            turn_x(1, t)
+        for t in range(2):
+            turn_back(0, t, True)
+        for t in range(4, 8):
+            row_norm(t)
+        for t in range(1, 5):
+            take_x(1, t, "s")
+        norm_extremes()
+        quantize_w(1, 1)
+        quantize_x(1, 0)
+        spread_extremes()
+        for t in range(5, 7):
+            turn_x(1, t)
+        for t in range(2, 6):
+            turn_back(0, t, True)
+        for t in range(5, 7):
+            take_x(1, t, "s")
+        noise_factor()
+        quantize_x(1, 1)
+        for t in range(4):
+            add_noise(t)
+        quantize_x(1, 2)
+        for t in range(4, 6):
+            add_noise(t)
+
+        for h in range(NH):
+            project(1, (0, 1), h)
+        turn_x(1, 7)
+        for t in range(6, 8):
+            turn_back(0, t, True)
+        for h in range(NH):
+            add_bias(1, (0, 1), h, "s")
+        take_x(1, 7, "s")
+        add_noise(6)
+        quantize_x(1, 3)
+        add_noise(7)
+        for t in range(4):
+            turn_back(1, t, False)
+        for h in range(NH):
+            project(1, (2, 3), h)
+        for h in range(NH):
+            add_bias(1, (2, 3), h, "s")
+        for t in range(4):
+            fuse(t)
+        for j in range(2):
+            partial_amax(pads[:, j : j + 1], j, 0, 2 * H)
+        for j in range(2):
+            store_out0(j)
+        for t in range(4, 8):
+            turn_back(1, t, False)
+        for t in range(4, 8):
+            fuse(t)
+        partial_amax(pads[:, 2:3], 2, 0, 2 * H)
+        partial_amax(am[:, 1:2], 3, 0, H)
+        partial_amax(am[:, 0:1], 3, H, 2 * H + PADS)
+        for j in range(2, 4):
+            store_out0(j)
+
+        spread_amax()
+        cast_factor()
+        for j in range(2):
+            cast(j, 0, 2 * H, "v")
         cast(3, 0, H, "v")
-        store8(0)
-        store8(1)
+        for j in range(2):
+            store_out1(j)
         cast(2, 0, H, "s")
-        cast(2, H, 2 * H, "s")
-        cast(3, H, 2 * H, "s")
-        store8(2)
-        store8(3)
+        for j in range(2, 4):
+            cast(j, H, 2 * H, "s")
+        for j in range(2, 4):
+            store_out1(j)

@@ -89,6 +89,9 @@ def tile_splitnn_pa_kernel(tc, x1, x2, W1, b1, W2, b2, noise_std, rr_uniform, ou
         cs = [None] * NT
         for t in range(NT):
             cs[t] = keep.tile([P, H], F32, name="cs%d" % t)
+        aks = {}
+        for t in (6, 7):
+            aks[t] = keep.tile([P, H], F32, name="aks%d" % t)
         outs = [None] * NJ
         o8 = [None] * NJ
         for j in range(NJ):
@@ -105,8 +108,10 @@ def tile_splitnn_pa_kernel(tc, x1, x2, W1, b1, W2, b2, noise_std, rr_uniform, ou
         nc.scalar.activation(out=warm[:], in_=zero[:], func=ACT.Abs)
         nc.vector.memset(vrow[:], 0.0)
         nc.vector.memset(pads, 0.0)
-        for i, vec in enumerate((b1, b2, rr_uniform)):
-            nc.sync.dma_start(out=vrow[NH * i : NH * (i + 1), :], in_=vec.rearrange("(h p) -> h p", p=P))
+
+        def load_vec():
+            for i, vec in enumerate((b1, b2, rr_uniform)):
+                nc.sync.dma_start(out=vrow[NH * i : NH * (i + 1), :], in_=vec.rearrange("(h p) -> h p", p=P))
 
         def load_w(c, g):
             nc.sync.dma_start(
@@ -118,30 +123,24 @@ def tile_splitnn_pa_kernel(tc, x1, x2, W1, b1, W2, b2, noise_std, rr_uniform, ou
                 out=xraw[c][j][:], in_=xs_in[c].rearrange("(p t) k -> p t k", t=NT)[:, 2 * j : 2 * j + 2, :]
             )
 
+        def load_xt(c, t):
+            nc.sync.dma_start(out=xraw[c][t // 2][:, t % 2, :], in_=xs_in[c].rearrange("(p t) k -> p t k", t=NT)[:, t, :])
+
         def load_noise(i):
             nc.sync.dma_start(out=noise[:, 4 * i : 4 * i + 4, :], in_=noise_v[:, 4 * i : 4 * i + 4, :])
 
-        for g in range(NG):
-            load_w(0, g)
-        for j in range(NJ):
-            load_x(0, j)
-        for g in range(NG):
-            load_w(1, g)
-        for i in range(2):
-            load_x(1, 2 * i)
-            load_x(1, 2 * i + 1)
-            load_noise(i)
-
         def widen_vectors():
-            nc.vector.tensor_copy(out=vrow32[:], in_=vrow[:])
+            nc.gpsimd.tensor_copy(out=vrow32[:], in_=vrow[:])
 
         def turn_vectors():
             ps["vec"] = bank()
             nc.tensor.transpose(ps["vec"][:, 0:P], vrow32[:], ident[:])
 
         def take_vectors():
-            nc.vector.tensor_copy(out=vcol[:], in_=ps["vec"][:, 0 : 3 * NH])
-            nc.vector.tensor_scalar(out=kcol[:], in0=vcol[:, 2 * NH : 3 * NH], scalar1=P_KEEP, scalar2=None, op0=ALU.is_lt)
+            nc.scalar.copy(out=vcol[:], in_=ps["vec"][:, 0 : 3 * NH])
+
+        def make_kcol():
+            nc.gpsimd.tensor_scalar(out=kcol[:], in0=vcol[:, 2 * NH : 3 * NH], scalar1=P_KEEP, scalar2=None, op0=ALU.is_lt)
 
         def mask_identities():
             for h in range(NH):
@@ -264,6 +263,15 @@ def tile_splitnn_pa_kernel(tc, x1, x2, W1, b1, W2, b2, noise_std, rr_uniform, ou
                 out=cs[t][:], in0=nk[:, t, :], scalar=nmul[:, 0:1], in1=ps["back", 0, t, True][:], op0=ALU.mult, op1=ALU.add
             )
 
+        def take_masked(t):
+            nc.scalar.copy(out=aks[t][:], in_=ps["back", 0, t, True][:])
+
+        def scale_noise(t):
+            nc.scalar.activation(out=cs[t][:], in_=nk[:, t, :], func=ACT.Copy, scale=nmul[:, 0:1])
+
+        def add_noise_g(t):
+            nc.gpsimd.tensor_tensor(out=cs[t][:], in0=cs[t][:], in1=aks[t][:], op=ALU.add)
+
         def fuse(t):
             nc.vector.tensor_tensor(
                 out=outs[t // 2][:, (t % 2) * H : (t % 2 + 1) * H], in0=cs[t][:], in1=ps["back", 1, t, False][:], op=ALU.min
@@ -271,6 +279,12 @@ def tile_splitnn_pa_kernel(tc, x1, x2, W1, b1, W2, b2, noise_std, rr_uniform, ou
 
         def partial_amax(dst, j, lo, hi):
             nc.vector.tensor_reduce(out=dst, in_=outs[j][:, lo:hi], axis=AX.X, op=ALU.max, apply_absolute_value=True)
+
+        def amax_pad(k, j, lo, hi):
+            partial_amax(pads[:, k : k + 1], j, lo, hi)
+
+        def amax_col(k, j, lo, hi):
+            partial_amax(am[:, k : k + 1], j, lo, hi)
 
         def store_out0(j):
             nc.sync.dma_start(out=out0_v[:, 2 * j : 2 * j + 2, :], in_=outs[j][:, 0 : 2 * H].rearrange("p (t h) -> p t h", t=2))
@@ -300,132 +314,152 @@ def tile_splitnn_pa_kernel(tc, x1, x2, W1, b1, W2, b2, noise_std, rr_uniform, ou
         def store_out1(j):
             nc.sync.dma_start(out=out1_v[:, 2 * j : 2 * j + 2, :], in_=o8[j][:].bitcast(U8).rearrange("p (t h) -> p t h", t=2))
 
-
-        interleave_w(0, 1, "s", 0, W_SPLIT)
-        interleave_w(0, 0, "v", 0, H)
+        load_w(0, 0)
+        load_vec()
+        load_w(0, 1)
+        for i in range(8):
+            load_xt(0, i)
+        load_w(1, 0)
+        load_noise(0)
+        load_x(1, 0)
+        load_w(1, 1)
+        for i in range(1, 3):
+            load_x(1, i)
+        load_noise(1)
+        load_x(1, 3)
         widen_vectors()
         turn_vectors()
-        for t in range(4):
-            turn_x(0, t)
-        for t in range(4):
-            take_x(0, t, "s")
+        for i in range(4):
+            turn_x(0, i)
+        for i in range(2):
+            interleave_w(0, i, "s", 0, 192)
         take_vectors()
-        interleave_w(0, 1, "v", W_SPLIT, H)
-        for g in range(NG):
-            quantize_w(0, g)
-        for j in range(2):
-            quantize_x(0, j)
+        take_x(0, 1, "s")
+        take_x(0, 3, "s")
+        for i in range(2):
+            interleave_w(0, i, "v", 192, 512)
+        quantize_w(0, 0)
+        take_x(0, 0, "v")
+        quantize_w(0, 1)
+        take_x(0, 2, "v")
+        for i in range(2):
+            quantize_x(0, i)
+        make_kcol()
         mask_identities()
-
         spread_keep()
-        for t in range(4, 8):
-            turn_x(0, t)
-        for h in range(NH):
-            project(0, (0, 1), h)
-        turn_x(1, 0)
-        for t in range(4, 8):
-            take_x(0, t, "s")
+        for i in range(4, 8):
+            turn_x(0, i)
+        for i in range(4):
+            project(0, (0, 1), i)
+        for i in range(4, 6):
+            take_x(0, i, "s")
         take_keep()
-        for h in range(3):
-            add_bias(0, (0, 1), h, "s")
+        take_x(0, 7, "s")
+        for i in range(3):
+            add_bias(0, (0, 1), i, "s")
+        take_x(0, 6, "v")
         quantize_x(0, 2)
-        interleave_w(1, 0, "v", 0, H)
-        add_bias(0, (0, 1), 3, "v")
+        interleave_w(1, 0, "v", 0, 512)
         quantize_x(0, 3)
+        add_bias(0, (0, 1), 3, "v")
         quantize_w(1, 0)
-        mask_noise(0)
-
-        for h in range(2):
-            project(0, (2,), h)
-        for t in range(4):
-            turn_back(0, t, False)
-        for h in range(2, 4):
-            project(0, (2,), h)
-        for h in range(NH):
-            project(0, (3,), h)
-        for h in range(2):
-            add_bias(0, (2,), h, "s")
-        for t in range(4):
-            row_norm(t)
+        for i in range(3):
+            project(0, (2,), i)
+        turn_x(1, 0)
+        for i in range(4):
+            turn_back(0, i, False)
+        project(0, (2,), 3)
+        for i in range(4):
+            project(0, (3,), i)
+        for i in range(1, 3):
+            add_bias(0, (2,), i, "s")
+        for i in range(4):
+            row_norm(i)
         add_bias(0, (3,), 0, "s")
-        for h in range(2, 4):
-            add_bias(0, (2,), h, "v")
-        for h in range(1, 4):
-            add_bias(0, (3,), h, "v")
-        interleave_w(1, 1, "v", 0, H)
+        add_bias(0, (2,), 0, "v")
+        mask_noise(0)
+        add_bias(0, (2,), 3, "v")
         take_x(1, 0, "v")
+        for i in range(1, 4):
+            add_bias(0, (3,), i, "v")
+        interleave_w(1, 1, "v", 0, 512)
         mask_noise(1)
-
-        for t in range(4, 8):
-            turn_back(0, t, False)
-        for t in range(1, 5):
-            turn_x(1, t)
-        for t in range(2):
-            turn_back(0, t, True)
-        for t in range(4, 8):
-            row_norm(t)
-        for t in range(1, 5):
-            take_x(1, t, "s")
+        for i in range(4, 6):
+            turn_back(0, i, False)
+        turn_x(1, 1)
+        for i in range(6, 8):
+            turn_back(0, i, False)
+        for i in range(2, 4):
+            turn_x(1, i)
+        turn_back(0, 0, True)
+        turn_x(1, 4)
+        turn_back(0, 1, True)
+        turn_x(1, 5)
+        for i in range(4, 8):
+            row_norm(i)
+        for i in range(1, 6):
+            take_x(1, i, "s")
         norm_extremes()
         quantize_w(1, 1)
         quantize_x(1, 0)
         spread_extremes()
-        for t in range(5, 7):
-            turn_x(1, t)
-        for t in range(2, 6):
-            turn_back(0, t, True)
-        for t in range(5, 7):
-            take_x(1, t, "s")
+        for i in range(2, 4):
+            turn_back(0, i, True)
+        turn_x(1, 6)
+        for i in range(4, 6):
+            turn_back(0, i, True)
+        take_x(1, 6, "s")
         noise_factor()
         quantize_x(1, 1)
-        for t in range(4):
-            add_noise(t)
+        for i in range(5):
+            add_noise(i)
         quantize_x(1, 2)
-        for t in range(4, 6):
-            add_noise(t)
-
-        for h in range(NH):
-            project(1, (0, 1), h)
+        add_noise(5)
+        for i in range(4):
+            project(1, (0, 1), i)
         turn_x(1, 7)
-        for t in range(6, 8):
-            turn_back(0, t, True)
-        for h in range(NH):
-            add_bias(1, (0, 1), h, "s")
+        for i in range(6, 8):
+            turn_back(0, i, True)
+        for i in range(4):
+            add_bias(1, (0, 1), i, "s")
         take_x(1, 7, "s")
-        add_noise(6)
+        for i in range(6, 8):
+            take_masked(i)
+        scale_noise(6)
         quantize_x(1, 3)
-        add_noise(7)
-        for t in range(4):
-            turn_back(1, t, False)
-        for h in range(NH):
-            project(1, (2, 3), h)
-        for h in range(NH):
-            add_bias(1, (2, 3), h, "s")
-        for t in range(4):
-            fuse(t)
-        for j in range(2):
-            partial_amax(pads[:, j : j + 1], j, 0, 2 * H)
-        for j in range(2):
-            store_out0(j)
-        for t in range(4, 8):
-            turn_back(1, t, False)
-        for t in range(4, 8):
-            fuse(t)
-        partial_amax(pads[:, 2:3], 2, 0, 2 * H)
-        partial_amax(am[:, 1:2], 3, 0, H)
-        partial_amax(am[:, 0:1], 3, H, 2 * H + PADS)
-        for j in range(2, 4):
-            store_out0(j)
-
+        add_noise_g(6)
+        for i in range(4):
+            turn_back(1, i, False)
+        for i in range(4):
+            project(1, (2, 3), i)
+        for i in range(4):
+            add_bias(1, (2, 3), i, "s")
+        scale_noise(7)
+        for i in range(4):
+            fuse(i)
+        amax_pad(0, 0, 0, 1024)
+        amax_pad(1, 1, 0, 1024)
+        for i in range(2):
+            store_out0(i)
+        add_noise_g(7)
+        for i in range(4, 8):
+            turn_back(1, i, False)
+        for i in range(4, 8):
+            fuse(i)
+        amax_pad(2, 2, 0, 1024)
+        amax_col(1, 3, 0, 512)
+        amax_col(0, 3, 512, 1032)
+        for i in range(2, 4):
+            store_out0(i)
         spread_amax()
         cast_factor()
-        for j in range(2):
-            cast(j, 0, 2 * H, "v")
-        cast(3, 0, H, "v")
-        for j in range(2):
-            store_out1(j)
-        cast(2, 0, H, "s")
-        for j in range(2, 4):
-            cast(j, H, 2 * H, "s")
-        for j in range(2, 4):
-            store_out1(j)
+        for i in range(2):
+            cast(i, 0, 1024, "v")
+        cast(3, 0, 512, "v")
+        for i in range(2):
+            store_out1(i)
+        cast(2, 0, 512, "s")
+        for i in range(2, 4):
+            cast(i, 512, 1024, "s")
+        for i in range(2, 4):
+            store_out1(i)

@@ -90,7 +90,7 @@ def tile_splitnn_pa_kernel(tc, x1, x2, W1, b1, W2, b2, noise_std, rr_uniform, ou
         for t in range(NT):
             cs[t] = keep.tile([P, H], F32, name="cs%d" % t)
         aks = {}
-        for t in (6, 7):
+        for t in (5, 6, 7):
             aks[t] = keep.tile([P, H], F32, name="aks%d" % t)
         outs = [None] * NJ
         o8 = [None] * NJ
@@ -269,6 +269,9 @@ def tile_splitnn_pa_kernel(tc, x1, x2, W1, b1, W2, b2, noise_std, rr_uniform, ou
         def scale_noise(t):
             nc.scalar.activation(out=cs[t][:], in_=nk[:, t, :], func=ACT.Copy, scale=nmul[:, 0:1])
 
+        def scale_noise_g(t):
+            nc.gpsimd.tensor_scalar(out=cs[t][:], in0=nk[:, t, :], scalar1=nmul[:, 0:1], scalar2=0.0, op0=ALU.mult, op1=ALU.add)
+
         def add_noise_g(t):
             nc.gpsimd.tensor_tensor(out=cs[t][:], in0=cs[t][:], in1=aks[t][:], op=ALU.add)
 
@@ -411,10 +414,13 @@ def tile_splitnn_pa_kernel(tc, x1, x2, W1, b1, W2, b2, noise_std, rr_uniform, ou
         take_x(1, 6, "s")
         noise_factor()
         quantize_x(1, 1)
-        for i in range(5):
+        for i in range(3):
             add_noise(i)
         quantize_x(1, 2)
-        add_noise(5)
+        for i in range(3, 5):
+            add_noise(i)
+        for i in range(5, 8):
+            scale_noise_g(i)
         for i in range(4):
             project(1, (0, 1), i)
         turn_x(1, 7)
@@ -423,25 +429,23 @@ def tile_splitnn_pa_kernel(tc, x1, x2, W1, b1, W2, b2, noise_std, rr_uniform, ou
         for i in range(4):
             add_bias(1, (0, 1), i, "s")
         take_x(1, 7, "s")
-        for i in range(6, 8):
+        for i in range(5, 8):
             take_masked(i)
-        scale_noise(6)
         quantize_x(1, 3)
-        add_noise_g(6)
+        for i in range(5, 8):
+            add_noise_g(i)
         for i in range(4):
             turn_back(1, i, False)
         for i in range(4):
             project(1, (2, 3), i)
         for i in range(4):
             add_bias(1, (2, 3), i, "s")
-        scale_noise(7)
         for i in range(4):
             fuse(i)
         amax_pad(0, 0, 0, 1024)
         amax_pad(1, 1, 0, 1024)
         for i in range(2):
             store_out0(i)
-        add_noise_g(7)
         for i in range(4, 8):
             turn_back(1, i, False)
         for i in range(4, 8):

@@ -90,7 +90,7 @@ def tile_splitnn_pa_kernel(tc, x1, x2, W1, b1, W2, b2, noise_std, rr_uniform, ou
         for t in range(NT):
             cs[t] = keep.tile([P, H], F32, name="cs%d" % t)
         aks = {}
-        for t in (5, 6, 7):
+        for t in (4, 5, 6, 7):
             aks[t] = keep.tile([P, H], F32, name="aks%d" % t)
         outs = [None] * NJ
         o8 = [None] * NJ
@@ -394,67 +394,92 @@ def tile_splitnn_pa_kernel(tc, x1, x2, W1, b1, W2, b2, noise_std, rr_uniform, ou
             turn_back(0, i, False)
         for i in range(2, 4):
             turn_x(1, i)
-        turn_back(0, 0, True)
+        for i in range(2):
+            turn_back(0, i, True)
         turn_x(1, 4)
-        turn_back(0, 1, True)
-        turn_x(1, 5)
+        turn_back(0, 2, True)
         for i in range(4, 8):
             row_norm(i)
-        for i in range(1, 6):
+        for i in range(1, 5):
             take_x(1, i, "s")
         norm_extremes()
         quantize_w(1, 1)
         quantize_x(1, 0)
         spread_extremes()
-        for i in range(2, 4):
-            turn_back(0, i, True)
-        turn_x(1, 6)
-        for i in range(4, 6):
-            turn_back(0, i, True)
-        take_x(1, 6, "s")
+        turn_x(1, 5)
+        turn_back(0, 3, True)
+        for i in range(4):
+            project(1, (0,), i)
+        take_x(1, 5, "s")
+        for i in range(4):
+            add_bias(1, (0,), i, "s")
         noise_factor()
         quantize_x(1, 1)
-        for i in range(3):
-            add_noise(i)
+        add_noise(0)
         quantize_x(1, 2)
-        for i in range(3, 5):
+        for i in range(1, 4):
             add_noise(i)
-        for i in range(5, 8):
+        for i in range(4, 8):
             scale_noise_g(i)
         for i in range(4):
-            project(1, (0, 1), i)
+            project(1, (1,), i)
+        turn_x(1, 6)
+        for i in range(2):
+            turn_back(1, i, False)
         turn_x(1, 7)
+        for i in range(4):
+            project(1, (2,), i)
+        for i in range(4, 6):
+            turn_back(0, i, True)
+        for i in range(2):
+            add_bias(1, (1,), i, "s")
+        take_x(1, 6, "s")
+        for i in range(2, 4):
+            add_bias(1, (1,), i, "s")
+        take_x(1, 7, "s")
+        for i in range(2):
+            add_bias(1, (2,), i, "s")
+        for i in range(4, 6):
+            take_masked(i)
+        for i in range(2, 4):
+            add_bias(1, (2,), i, "s")
+        for i in range(2):
+            fuse(i)
+        quantize_x(1, 3)
+        amax_pad(0, 0, 0, 1024)
+        store_out0(0)
+        for i in range(4, 6):
+            add_noise_g(i)
+        for i in range(2, 4):
+            turn_back(1, i, False)
         for i in range(6, 8):
             turn_back(0, i, True)
         for i in range(4):
-            add_bias(1, (0, 1), i, "s")
-        take_x(1, 7, "s")
-        for i in range(5, 8):
-            take_masked(i)
-        quantize_x(1, 3)
-        for i in range(5, 8):
-            add_noise_g(i)
-        for i in range(4):
+            project(1, (3,), i)
+        for i in range(4, 6):
             turn_back(1, i, False)
-        for i in range(4):
-            project(1, (2, 3), i)
-        for i in range(4):
-            add_bias(1, (2, 3), i, "s")
-        for i in range(4):
+        take_masked(6)
+        add_bias(1, (3,), 0, "s")
+        take_masked(7)
+        for i in range(1, 4):
+            add_bias(1, (3,), i, "s")
+        for i in range(2, 4):
             fuse(i)
-        amax_pad(0, 0, 0, 1024)
         amax_pad(1, 1, 0, 1024)
-        for i in range(2):
-            store_out0(i)
-        for i in range(4, 8):
-            turn_back(1, i, False)
-        for i in range(4, 8):
+        for i in range(4, 6):
             fuse(i)
         amax_pad(2, 2, 0, 1024)
+        for i in range(1, 3):
+            store_out0(i)
+        for i in range(6, 8):
+            add_noise_g(i)
+        for i in range(6, 8):
+            turn_back(1, i, False)
+        for i in range(6, 8):
+            fuse(i)
         amax_col(1, 3, 0, 512)
         amax_col(0, 3, 512, 1032)
-        for i in range(2, 4):
-            store_out0(i)
+        store_out0(3)
         spread_amax()
         cast_factor()
         for i in range(2):

@@ -337,14 +337,12 @@ def tile_splitnn_pa_kernel(tc, x1, x2, W1, b1, W2, b2, noise_std, rr_uniform, ou
         for i in range(2):
             interleave_w(0, i, "s", 0, 192)
         take_vectors()
-        take_x(0, 1, "s")
-        take_x(0, 3, "s")
+        for i in range(4):
+            take_x(0, i, "s")
         for i in range(2):
             interleave_w(0, i, "v", 192, 512)
-        quantize_w(0, 0)
-        take_x(0, 0, "v")
-        quantize_w(0, 1)
-        take_x(0, 2, "v")
+        for i in range(2):
+            quantize_w(0, i)
         for i in range(2):
             quantize_x(0, i)
         make_kcol()
@@ -366,6 +364,7 @@ def tile_splitnn_pa_kernel(tc, x1, x2, W1, b1, W2, b2, noise_std, rr_uniform, ou
         quantize_x(0, 3)
         add_bias(0, (0, 1), 3, "v")
         quantize_w(1, 0)
+        mask_noise(0)
         for i in range(3):
             project(0, (2,), i)
         turn_x(1, 0)
@@ -374,13 +373,11 @@ def tile_splitnn_pa_kernel(tc, x1, x2, W1, b1, W2, b2, noise_std, rr_uniform, ou
         project(0, (2,), 3)
         for i in range(4):
             project(0, (3,), i)
-        for i in range(1, 3):
+        for i in range(3):
             add_bias(0, (2,), i, "s")
         for i in range(4):
             row_norm(i)
         add_bias(0, (3,), 0, "s")
-        add_bias(0, (2,), 0, "v")
-        mask_noise(0)
         add_bias(0, (2,), 3, "v")
         take_x(1, 0, "v")
         for i in range(1, 4):
@@ -427,26 +424,25 @@ def tile_splitnn_pa_kernel(tc, x1, x2, W1, b1, W2, b2, noise_std, rr_uniform, ou
         for i in range(2):
             turn_back(1, i, False)
         turn_x(1, 7)
-        for i in range(4):
-            project(1, (2,), i)
         for i in range(4, 6):
             turn_back(0, i, True)
+        for i in range(4):
+            project(1, (2,), i)
         for i in range(2):
             add_bias(1, (1,), i, "s")
         take_x(1, 6, "s")
         for i in range(2, 4):
             add_bias(1, (1,), i, "s")
         take_x(1, 7, "s")
-        for i in range(2):
-            add_bias(1, (2,), i, "s")
         for i in range(4, 6):
             take_masked(i)
-        for i in range(2, 4):
+        for i in range(4):
             add_bias(1, (2,), i, "s")
         for i in range(2):
             fuse(i)
+        amax_pad(0, 0, 0, 512)
         quantize_x(1, 3)
-        amax_pad(0, 0, 0, 1024)
+        amax_pad(1, 0, 512, 1024)
         store_out0(0)
         for i in range(4, 6):
             add_noise_g(i)
@@ -465,10 +461,12 @@ def tile_splitnn_pa_kernel(tc, x1, x2, W1, b1, W2, b2, noise_std, rr_uniform, ou
             add_bias(1, (3,), i, "s")
         for i in range(2, 4):
             fuse(i)
-        amax_pad(1, 1, 0, 1024)
+        amax_pad(2, 1, 0, 512)
+        amax_pad(3, 1, 512, 1024)
         for i in range(4, 6):
             fuse(i)
-        amax_pad(2, 2, 0, 1024)
+        amax_pad(4, 2, 0, 512)
+        amax_pad(5, 2, 512, 1024)
         for i in range(1, 3):
             store_out0(i)
         for i in range(6, 8):

@@ -158,7 +158,9 @@ def tile_splitnn_pa_kernel(tc, x1, x2, W1, b1, W2, b2, noise_std, rr_uniform, ou
 
         def interleave_w(c, g, engine, lo, hi):
             src = wraw[c][g][:, :, lo:hi].rearrange("p e w -> p w e")
-            if engine == "s":
+            if engine == "g":
+                nc.gpsimd.tensor_scalar(out=wgrp[c][g][:, lo:hi, :], in0=src, scalar1=1.0, scalar2=0.0, op0=ALU.mult, op1=ALU.add)
+            elif engine == "s":
                 nc.scalar.copy(out=wgrp[c][g][:, lo:hi, :], in_=src)
             else:
                 nc.vector.tensor_copy(out=wgrp[c][g][:, lo:hi, :], in_=src)
@@ -347,6 +349,10 @@ def tile_splitnn_pa_kernel(tc, x1, x2, W1, b1, W2, b2, noise_std, rr_uniform, ou
             quantize_x(0, i)
         make_kcol()
         mask_identities()
+        interleave_w(1, 1, "g", 0, 128)
+        interleave_w(1, 1, "g", 128, 256)
+        interleave_w(1, 1, "g", 256, 384)
+        interleave_w(1, 1, "g", 384, 512)
         spread_keep()
         for i in range(4, 8):
             turn_x(0, i)
@@ -379,11 +385,9 @@ def tile_splitnn_pa_kernel(tc, x1, x2, W1, b1, W2, b2, noise_std, rr_uniform, ou
             row_norm(i)
         add_bias(0, (3,), 0, "s")
         add_bias(0, (2,), 3, "v")
-        take_x(1, 0, "v")
         for i in range(1, 4):
             add_bias(0, (3,), i, "v")
-        interleave_w(1, 1, "v", 0, 512)
-        mask_noise(1)
+        take_x(1, 0, "v")
         for i in range(4, 6):
             turn_back(0, i, False)
         turn_x(1, 1)
@@ -397,10 +401,12 @@ def tile_splitnn_pa_kernel(tc, x1, x2, W1, b1, W2, b2, noise_std, rr_uniform, ou
         turn_back(0, 2, True)
         for i in range(4, 8):
             row_norm(i)
-        for i in range(1, 5):
+        for i in range(2, 5):
             take_x(1, i, "s")
-        norm_extremes()
+        take_x(1, 1, "v")
+        mask_noise(1)
         quantize_w(1, 1)
+        norm_extremes()
         quantize_x(1, 0)
         spread_extremes()
         turn_x(1, 5)
@@ -450,10 +456,12 @@ def tile_splitnn_pa_kernel(tc, x1, x2, W1, b1, W2, b2, noise_std, rr_uniform, ou
             turn_back(1, i, False)
         for i in range(6, 8):
             turn_back(0, i, True)
-        for i in range(4):
+        for i in range(2):
             project(1, (3,), i)
         for i in range(4, 6):
             turn_back(1, i, False)
+        for i in range(2, 4):
+            project(1, (3,), i)
         take_masked(6)
         add_bias(1, (3,), 0, "s")
         take_masked(7)

@@ -271,6 +271,9 @@ def tile_splitnn_pa_kernel(tc, x1, x2, W1, b1, W2, b2, noise_std, rr_uniform, ou
         def scale_noise(t):
             nc.scalar.activation(out=cs[t][:], in_=nk[:, t, :], func=ACT.Copy, scale=nmul[:, 0:1])
 
+        def mask_noise_g(t):
+            nc.gpsimd.tensor_tensor(out=nk[:, t, :], in0=noise[:, t, :], in1=keepb[:], op=ALU.mult)
+
         def scale_noise_g(t):
             nc.gpsimd.tensor_scalar(out=cs[t][:], in0=nk[:, t, :], scalar1=nmul[:, 0:1], scalar2=0.0, op0=ALU.mult, op1=ALU.add)
 
@@ -333,54 +336,52 @@ def tile_splitnn_pa_kernel(tc, x1, x2, W1, b1, W2, b2, noise_std, rr_uniform, ou
         load_noise(1)
         load_x(1, 3)
         widen_vectors()
+        for i in range(6):
+            turn_x(0, i)
         turn_vectors()
-        for i in range(4):
+        for i in range(6, 8):
             turn_x(0, i)
         for i in range(2):
             interleave_w(0, i, "s", 0, 192)
-        take_vectors()
-        for i in range(4):
+        for i in range(6):
             take_x(0, i, "s")
+        take_vectors()
+        take_x(0, 7, "s")
         for i in range(2):
             interleave_w(0, i, "v", 192, 512)
         for i in range(2):
             quantize_w(0, i)
         for i in range(2):
             quantize_x(0, i)
+        take_x(0, 6, "v")
+        quantize_x(0, 2)
+        interleave_w(1, 0, "v", 0, 512)
+        quantize_x(0, 3)
         make_kcol()
         mask_identities()
         interleave_w(1, 1, "g", 0, 128)
         interleave_w(1, 1, "g", 128, 256)
         interleave_w(1, 1, "g", 256, 384)
         interleave_w(1, 1, "g", 384, 512)
-        spread_keep()
-        for i in range(4, 8):
-            turn_x(0, i)
         for i in range(4):
             project(0, (0, 1), i)
-        for i in range(4, 6):
-            take_x(0, i, "s")
-        take_keep()
-        take_x(0, 7, "s")
+        for i in range(3):
+            project(0, (2,), i)
+        spread_keep()
+        turn_x(1, 0)
         for i in range(3):
             add_bias(0, (0, 1), i, "s")
-        take_x(0, 6, "v")
-        quantize_x(0, 2)
-        interleave_w(1, 0, "v", 0, 512)
-        quantize_x(0, 3)
+        for i in range(3):
+            add_bias(0, (2,), i, "s")
+        take_keep()
         add_bias(0, (0, 1), 3, "v")
         quantize_w(1, 0)
         mask_noise(0)
-        for i in range(3):
-            project(0, (2,), i)
-        turn_x(1, 0)
         for i in range(4):
             turn_back(0, i, False)
         project(0, (2,), 3)
         for i in range(4):
             project(0, (3,), i)
-        for i in range(3):
-            add_bias(0, (2,), i, "s")
         for i in range(4):
             row_norm(i)
         add_bias(0, (3,), 0, "s")

@@ -83,6 +83,7 @@ def tile_splitnn_pa_kernel(tc, x1, x2, W1, b1, W2, b2, noise_std, rr_uniform, ou
                 xgrp[c][j] = keep.tile([P, NG, PAIR, 4], BF16, name="xgrp%d%d" % (c, j), align_bytes=64)
                 xcodes[c][j] = keep.tile([P, NG, PAIR], U32, name="xcodes%d%d" % (c, j), align_bytes=64)
                 xscales[c][j] = keep.tile([P, NG, PAIR], U8, name="xscales%d%d" % (c, j), align_bytes=64)
+        still = keep.tile([P, BANK], F32, name="still")
         junk = [None] * 2
         for i in range(2):
             junk[i] = keep.tile([P, H], BF16, name="junk%d" % i)
@@ -108,6 +109,7 @@ def tile_splitnn_pa_kernel(tc, x1, x2, W1, b1, W2, b2, noise_std, rr_uniform, ou
         nc.scalar.activation(out=warm[:], in_=zero[:], func=ACT.Abs)
         nc.vector.memset(vrow[:], 0.0)
         nc.vector.memset(pads, 0.0)
+        nc.vector.memset(still[:], 0.0)
 
         def load_vec():
             for i, vec in enumerate((b1, b2, rr_uniform)):
@@ -131,6 +133,9 @@ def tile_splitnn_pa_kernel(tc, x1, x2, W1, b1, W2, b2, noise_std, rr_uniform, ou
 
         def widen_vectors():
             nc.gpsimd.tensor_copy(out=vrow32[:], in_=vrow[:])
+
+        def keep_warm(n):
+            nc.tensor.matmul(bank()[:, 0:n], lhsT=still[:, 0:P], rhs=still[:, 0:n], start=True, stop=True)
 
         def turn_vectors():
             ps["vec"] = bank()
@@ -336,11 +341,16 @@ def tile_splitnn_pa_kernel(tc, x1, x2, W1, b1, W2, b2, noise_std, rr_uniform, ou
         load_noise(1)
         load_x(1, 3)
         widen_vectors()
-        for i in range(6):
-            turn_x(0, i)
+        for i in range(2):
+            keep_warm(BANK)
+        for i in range(3):
+            turn_x(0, 2 * i)
+            turn_x(0, 2 * i + 1)
+            keep_warm(P)
         turn_vectors()
         for i in range(6, 8):
             turn_x(0, i)
+        keep_warm(P)
         for i in range(2):
             interleave_w(0, i, "s", 0, 192)
         for i in range(6):
@@ -394,10 +404,12 @@ def tile_splitnn_pa_kernel(tc, x1, x2, W1, b1, W2, b2, noise_std, rr_uniform, ou
         turn_x(1, 1)
         for i in range(6, 8):
             turn_back(0, i, False)
+        keep_warm(P)
         for i in range(2, 4):
             turn_x(1, i)
         for i in range(2):
             turn_back(0, i, True)
+        keep_warm(P)
         turn_x(1, 4)
         turn_back(0, 2, True)
         for i in range(4, 8):

from contextlib import ExitStack

import concourse.mybir as mybir
from concourse.masks import make_identity

F32 = mybir.dt.float32
BF16 = mybir.dt.bfloat16
U32 = mybir.dt.uint32
U8 = mybir.dt.uint8
FP8X4 = mybir.dt.float8_e4m3fn_x4
FP8 = mybir.dt.float8_e4m3fn
ALU = mybir.AluOpType
ACT = mybir.ActivationFunctionType
AX = mybir.AxisListType

P = 128
B, F, H = 1024, 1024, 512
K_PASS = 4 * P
NT = B // P
NJ = NT // 2
NG = F // K_PASS
NH = H // P
PAIR = 2 * P
BANK = 512
PADS = 8
P_KEEP = 0.95
INV_EPS = 7.5
FP8_MAX = 448.0
W_SPLIT = 192
FLOPS = 2 * 2 * B * F * H


def tile_splitnn_pa_kernel(tc, x1, x2, W1, b1, W2, b2, noise_std, rr_uniform, out_0, out_1):
    nc = tc.nc
    xs_in = (x1, x2)
    ws_in = (W1, W2)

    with ExitStack() as ctx:
        keep = ctx.enter_context(tc.tile_pool(name="keep", bufs=1))
        psum = ctx.enter_context(tc.psum_pool(name="psum", bufs=8))
        ctx.enter_context(tc.manual_schedule())

        def bank():
            t = psum.tile([P, BANK], F32, name="ps", tag="ps", bufs=8)
            return t

        ident = keep.tile([P, P], F32, name="ident")
        zero = keep.tile([P, 1], F32, name="zero")
        warm = keep.tile([P, 1], F32, name="warm")
        vrow = keep.tile([P, P], BF16, name="vrow")
        vrow32 = keep.tile([P, P], F32, name="vrow32")
        vcol = keep.tile([P, 3 * NH], F32, name="vcol")
        kcol = keep.tile([P, NH], F32, name="kcol")
        identk = keep.tile([P, NH, P], F32, name="identk")
        keepb = keep.tile([P, H], BF16, name="keepb")
        noise = keep.tile([P, NT, H], BF16, name="noise")
        nk = keep.tile([P, NT, H], BF16, name="nk")
        norms = keep.tile([P, NT], F32, name="norms")
        junk_n = keep.tile([P, NT], F32, name="junkn")
        junk_s = keep.tile([P, 2 * P], F32, name="junks")
        ext = keep.tile([P, 2], F32, name="ext")
        gext = keep.tile([P, 2], F32, name="gext")
        nmul = keep.tile([P, 1], F32, name="nmul")
        am = keep.tile([P, 4], F32, name="am")
        wraw = [[None] * NG for c in range(2)]
        wgrp = [[None] * NG for c in range(2)]
        xraw = [[None] * NJ for c in range(2)]
        xgrp = [[None] * NJ for c in range(2)]
        xcodes = [[None] * NJ for c in range(2)]
        xscales = [[None] * NJ for c in range(2)]
        wcodes = [None] * 2
        wscales = [None] * 2
        res_t = [None] * 2
        for c in range(2):
            wcodes[c] = keep.tile([P, NG, H], U32, name="wcodes%d" % c, align_bytes=64)
            wscales[c] = keep.tile([P, NG, H], U8, name="wscales%d" % c, align_bytes=64)
            res_t[c] = keep.tile([P, NH, B], F32, name="rest%d" % c)
            for g in range(NG):
                wraw[c][g] = keep.tile([P, 4, H], BF16, name="wraw%d%d" % (c, g))
                wgrp[c][g] = keep.tile([P, H, 4], BF16, name="wgrp%d%d" % (c, g), align_bytes=64)
            for j in range(NJ):
                xraw[c][j] = keep.tile([P, 2, F], BF16, name="xraw%d%d" % (c, j))
                xgrp[c][j] = keep.tile([P, NG, PAIR, 4], BF16, name="xgrp%d%d" % (c, j), align_bytes=64)
                xcodes[c][j] = keep.tile([P, NG, PAIR], U32, name="xcodes%d%d" % (c, j), align_bytes=64)
                xscales[c][j] = keep.tile([P, NG, PAIR], U8, name="xscales%d%d" % (c, j), align_bytes=64)
        still = keep.tile([P, BANK], F32, name="still")
        junk = [None] * 2
        for i in range(2):
            junk[i] = keep.tile([P, H], BF16, name="junk%d" % i)
        cs = [None] * NT
        for t in range(NT):
            cs[t] = keep.tile([P, H], F32, name="cs%d" % t)
        aks = {}
        for t in (4, 5, 6, 7):
            aks[t] = keep.tile([P, H], F32, name="aks%d" % t)
        outs = [None] * NJ
        o8 = [None] * NJ
        for j in range(NJ):
            outs[j] = keep.tile([P, 2 * H + (PADS if j == NJ - 1 else 0)], F32, name="outs%d" % j)
            o8[j] = keep.tile([P, 2 * H], FP8, name="o8%d" % j)
        pads = outs[NJ - 1][:, 2 * H : 2 * H + PADS]
        out0_v = out_0.rearrange("(p t) h -> p t h", t=NT)
        out1_v = out_1.rearrange("(p t) h -> p t h", t=NT)
        noise_v = noise_std.rearrange("(p t) h -> p t h", t=NT)
        ps = {}

        make_identity(nc, ident[:])
        nc.vector.memset(zero[:], 0.0)
        nc.scalar.activation(out=warm[:], in_=zero[:], func=ACT.Abs)
        nc.vector.memset(vrow[:], 0.0)
        nc.vector.memset(pads, 0.0)
        nc.vector.memset(still[:], 0.0)

        def load_vec():
            for i, vec in enumerate((b1, b2, rr_uniform)):
                nc.sync.dma_start(out=vrow[NH * i : NH * (i + 1), :], in_=vec.rearrange("(h p) -> h p", p=P))

        def load_w(c, g):
            nc.sync.dma_start(
                out=wraw[c][g][:], in_=ws_in[c][g * K_PASS : (g + 1) * K_PASS, :].rearrange("(p e) w -> p e w", e=4)
            )

        def load_x(c, j):
            nc.sync.dma_start(
                out=xraw[c][j][:], in_=xs_in[c].rearrange("(p t) k -> p t k", t=NT)[:, 2 * j : 2 * j + 2, :]
            )

        def load_xt(c, t):
            nc.sync.dma_start(out=xraw[c][t // 2][:, t % 2, :], in_=xs_in[c].rearrange("(p t) k -> p t k", t=NT)[:, t, :])

        def load_noise(i):
            nc.sync.dma_start(out=noise[:, 4 * i : 4 * i + 4, :], in_=noise_v[:, 4 * i : 4 * i + 4, :])

        def widen_vectors():
            nc.gpsimd.tensor_copy(out=vrow32[:], in_=vrow[:])

        def keep_warm(n):
            nc.tensor.matmul(bank()[:, 0:n], lhsT=still[:, 0:P], rhs=still[:, 0:n], start=True, stop=True)

        def turn_vectors():
            ps["vec"] = bank()
            nc.tensor.transpose(ps["vec"][:, 0:P], vrow32[:], ident[:])

        def take_vectors():
            nc.scalar.copy(out=vcol[:], in_=ps["vec"][:, 0 : 3 * NH])

        def make_kcol():
            nc.gpsimd.tensor_scalar(out=kcol[:], in0=vcol[:, 2 * NH : 3 * NH], scalar1=P_KEEP, scalar2=None, op0=ALU.is_lt)

        def mask_identities():
            for h in range(NH):
                nc.gpsimd.tensor_scalar(
                    out=identk[:, h, :], in0=ident[:], scalar1=kcol[:, h : h + 1], scalar2=0.0, op0=ALU.mult, op1=ALU.add
                )

        def spread_keep():
            ps["keep"] = bank()
            for h in range(NH):
                nc.tensor.transpose(ps["keep"][:, h * P : (h + 1) * P], kcol[:, h : h + 1].to_broadcast([P, P]), ident[:])

        def take_keep():
            nc.scalar.copy(out=keepb[:], in_=ps["keep"][:])

        def interleave_w(c, g, engine, lo, hi):
            src = wraw[c][g][:, :, lo:hi].rearrange("p e w -> p w e")
            if engine == "g":
                nc.gpsimd.tensor_scalar(out=wgrp[c][g][:, lo:hi, :], in0=src, scalar1=1.0, scalar2=0.0, op0=ALU.mult, op1=ALU.add)
            elif engine == "s":
                nc.scalar.copy(out=wgrp[c][g][:, lo:hi, :], in_=src)
            else:
                nc.vector.tensor_copy(out=wgrp[c][g][:, lo:hi, :], in_=src)

        def quantize_w(c, g):
            nc.vector.quantize_mx(
                out=wcodes[c][:, g, :].bitcast(FP8X4),
                scales=wscales[c][:, g, :],
                in_=wgrp[c][g][:].rearrange("p w e -> p (w e)"),
            )

        def turn_x(c, t):
            words = xraw[c][t // 2][:, t % 2, :].bitcast(F32)
            pt = psum.tile([P, 2 * NG, P], F32, name="ps", tag="ps", bufs=8)
            ps["x", c, t] = pt
            for g in range(NG):
                for u in range(2):
                    nc.tensor.transpose(pt[:, 2 * g + u, :], words[:, 256 * g + u : 256 * (g + 1) : 2], ident[:])

        def take_x(c, t, engine):
            i = t % 2
            dst = xgrp[c][t // 2][:].bitcast(F32)[:, :, i * P : (i + 1) * P, :]
            src = ps["x", c, t][:].rearrange("p (g u) r -> p g r u", g=NG)
            if engine == "s":
                nc.scalar.copy(out=dst, in_=src)
            else:
                nc.vector.tensor_copy(out=dst, in_=src)

        def quantize_x(c, j):
            nc.vector.quantize_mx(
                out=xcodes[c][j][:].rearrange("p g r -> p (g r)").bitcast(FP8X4),
                scales=xscales[c][j][:].rearrange("p g r -> p (g r)"),
                in_=xgrp[c][j][:].rearrange("p g r e -> p (g r e)"),
            )

        def project(c, pairs, h):
            acc = bank()
            ps["acc", c, pairs[0], h] = acc
            for i, j in enumerate(pairs):
                for g in range(NG):
                    nc.tensor.matmul_mx(
                        out=acc[:, i * PAIR : (i + 1) * PAIR],
                        lhsT=wcodes[c][:, g, h * P : (h + 1) * P].bitcast(FP8X4),
                        lhsT_scale=wscales[c][:, g, h * P : (h + 1) * P],
                        rhs=xcodes[c][j][:, g, :].bitcast(FP8X4),
                        rhs_scale=xscales[c][j][:, g, :],
                        start=(g == 0),
                        stop=(g == NG - 1),
                    )

        def add_bias(c, pairs, h, engine):
            src = ps["acc", c, pairs[0], h][:, 0 : PAIR * len(pairs)]
            dst = res_t[c][:, h, PAIR * pairs[0] : PAIR * (pairs[0] + len(pairs))]
            bias = vcol[:, NH * c + h : NH * c + h + 1]
            if engine == "s":
                nc.scalar.activation(out=dst, in_=src, func=ACT.Identity, bias=bias, scale=1.0)
            else:
                nc.vector.tensor_scalar(out=dst, in0=src, scalar1=bias, scalar2=None, op0=ALU.add)

        def turn_back(c, t, masked):
            pb = bank()
            ps["back", c, t, masked] = pb
            for h in range(NH):
                nc.tensor.transpose(
                    pb[:, h * P : (h + 1) * P], res_t[c][:, h, t * P : (t + 1) * P], identk[:, h, :] if masked else ident[:]
                )

        def row_norm(t):
            nc.scalar.activation(
                out=junk[t % 2][:], in_=ps["back", 0, t, False][:], func=ACT.Abs, accum_out=norms[:, t : t + 1]
            )

        def norm_extremes():
            nc.vector.tensor_reduce(out=ext[:, 0:1], in_=norms[:], axis=AX.X, op=ALU.max)
            nc.vector.tensor_scalar(
                out=junk_n[:], in0=norms[:], scalar1=-1.0, scalar2=None, op0=ALU.mult, op1=ALU.max, accum_out=ext[:, 1:2]
            )

        def spread_extremes():
            ps["ext"] = bank()
            for i in range(2):
                nc.tensor.transpose(ps["ext"][:, i * P : (i + 1) * P], ext[:, i : i + 1].to_broadcast([P, P]), ident[:])

        def noise_factor():
            nc.vector.tensor_reduce(
                out=gext[:], in_=ps["ext"][:, 0 : 2 * P].rearrange("p (i q) -> p i q", i=2), axis=AX.X, op=ALU.max
            )
            nc.vector.tensor_scalar(
                out=nmul[:], in0=gext[:, 0:1], scalar1=gext[:, 1:2], scalar2=INV_EPS, op0=ALU.add, op1=ALU.mult
            )

        def mask_noise(i):
            nc.vector.tensor_tensor(
                out=nk[:, 4 * i : 4 * i + 4, :],
                in0=noise[:, 4 * i : 4 * i + 4, :],
                in1=keepb[:].unsqueeze(1).to_broadcast([P, 4, H]),
                op=ALU.mult,
            )

        def add_noise(t):
            nc.vector.scalar_tensor_tensor(
                out=cs[t][:], in0=nk[:, t, :], scalar=nmul[:, 0:1], in1=ps["back", 0, t, True][:], op0=ALU.mult, op1=ALU.add
            )

        def take_masked(t):
            nc.scalar.copy(out=aks[t][:], in_=ps["back", 0, t, True][:])

        def scale_noise(t):
            nc.scalar.activation(out=cs[t][:], in_=nk[:, t, :], func=ACT.Copy, scale=nmul[:, 0:1])

        def mask_noise_g(t):
            nc.gpsimd.tensor_tensor(out=nk[:, t, :], in0=noise[:, t, :], in1=keepb[:], op=ALU.mult)

        def scale_noise_g(t):
            nc.gpsimd.tensor_scalar(out=cs[t][:], in0=nk[:, t, :], scalar1=nmul[:, 0:1], scalar2=0.0, op0=ALU.mult, op1=ALU.add)

        def add_noise_g(t):
            nc.gpsimd.tensor_tensor(out=cs[t][:], in0=cs[t][:], in1=aks[t][:], op=ALU.add)

        def fuse(t):
            nc.vector.tensor_tensor(
                out=outs[t // 2][:, (t % 2) * H : (t % 2 + 1) * H], in0=cs[t][:], in1=ps["back", 1, t, False][:], op=ALU.min
            )

        def partial_amax(dst, j, lo, hi):
            nc.vector.tensor_reduce(out=dst, in_=outs[j][:, lo:hi], axis=AX.X, op=ALU.max, apply_absolute_value=True)

        def amax_pad(k, j, lo, hi):
            partial_amax(pads[:, k : k + 1], j, lo, hi)

        def amax_col(k, j, lo, hi):
            partial_amax(am[:, k : k + 1], j, lo, hi)

        def store_out0(j):
            nc.sync.dma_start(out=out0_v[:, 2 * j : 2 * j + 2, :], in_=outs[j][:, 0 : 2 * H].rearrange("p (t h) -> p t h", t=2))

        def spread_amax():
            ps["amax"] = bank()
            for i in range(2):
                nc.tensor.transpose(ps["amax"][:, i * P : (i + 1) * P], am[:, i : i + 1].to_broadcast([P, P]), ident[:])

        def cast_factor():
            nc.vector.tensor_scalar(
                out=junk_s[:], in0=ps["amax"][:, 0 : 2 * P], scalar1=1.0 / FP8_MAX, scalar2=None, op0=ALU.mult, op1=ALU.max,
                accum_out=am[:, 2:3],
            )
            nc.vector.reciprocal(out=am[:, 3:4], in_=am[:, 2:3])

        def cast(j, lo, hi, engine):
            if engine == "s":
                nc.scalar.activation(
                    out=o8[j][:, lo:hi], in_=outs[j][:, lo:hi], func=ACT.Identity, scale=am[:, 3:4], bias=zero[:, 0:1], saturate=False
                )
            else:
                nc.vector.tensor_scalar(
                    out=o8[j][:, lo:hi], in0=outs[j][:, lo:hi], scalar1=am[:, 3:4], scalar2=None, op0=ALU.mult, saturate=False
                )

        def store_out1(j):
            nc.sync.dma_start(out=out1_v[:, 2 * j : 2 * j + 2, :], in_=o8[j][:].bitcast(U8).rearrange("p (t h) -> p t h", t=2))

        load_w(0, 0)
        load_vec()
        load_w(0, 1)
        for i in range(8):
            load_xt(0, i)
        load_w(1, 0)
        load_noise(0)
        load_x(1, 0)
        load_w(1, 1)
        for i in range(1, 3):
            load_x(1, i)
        load_noise(1)
        load_x(1, 3)
        widen_vectors()
        for i in range(2):
            keep_warm(BANK)
        for i in range(3):
            turn_x(0, 2 * i)
            turn_x(0, 2 * i + 1)
            keep_warm(P)
        turn_vectors()
        for i in range(6, 8):
            turn_x(0, i)
        keep_warm(P)
        for i in range(2):
            interleave_w(0, i, "s", 0, 192)
        for i in range(6):
            take_x(0, i, "s")
        take_vectors()
        take_x(0, 7, "s")
        for i in range(2):
            interleave_w(0, i, "v", 192, 512)
        for i in range(2):
            quantize_w(0, i)
        for i in range(2):
            quantize_x(0, i)
        take_x(0, 6, "v")
        quantize_x(0, 2)
        interleave_w(1, 0, "v", 0, 512)
        quantize_x(0, 3)
        make_kcol()
        mask_identities()
        interleave_w(1, 1, "g", 0, 128)
        interleave_w(1, 1, "g", 128, 256)
        interleave_w(1, 1, "g", 256, 384)
        interleave_w(1, 1, "g", 384, 512)
        for i in range(4):
            project(0, (0, 1), i)
        for i in range(3):
            project(0, (2,), i)
        spread_keep()
        turn_x(1, 0)
        for i in range(3):
            add_bias(0, (0, 1), i, "s")
        for i in range(3):
            add_bias(0, (2,), i, "s")
        take_keep()
        add_bias(0, (0, 1), 3, "v")
        quantize_w(1, 0)
        mask_noise(0)
        for i in range(4):
            turn_back(0, i, False)
        project(0, (2,), 3)
        for i in range(4):
            project(0, (3,), i)
        for i in range(4):
            row_norm(i)
        add_bias(0, (3,), 0, "s")
        add_bias(0, (2,), 3, "v")
        for i in range(1, 4):
            add_bias(0, (3,), i, "v")
        take_x(1, 0, "v")
        for i in range(4, 6):
            turn_back(0, i, False)
        turn_x(1, 1)
        for i in range(6, 8):
            turn_back(0, i, False)
        keep_warm(P)
        for i in range(2, 4):
            turn_x(1, i)
        for i in range(2):
            turn_back(0, i, True)
        keep_warm(P)
        turn_x(1, 4)
        turn_back(0, 2, True)
        for i in range(4, 8):
            row_norm(i)
        for i in range(2, 5):
            take_x(1, i, "s")
        take_x(1, 1, "v")
        mask_noise(1)
        quantize_w(1, 1)
        norm_extremes()
        quantize_x(1, 0)
        spread_extremes()
        turn_x(1, 5)
        turn_back(0, 3, True)
        for i in range(4):
            project(1, (0,), i)
        take_x(1, 5, "s")
        for i in range(4):
            add_bias(1, (0,), i, "s")
        noise_factor()
        quantize_x(1, 1)
        add_noise(0)
        quantize_x(1, 2)
        for i in range(1, 4):
            add_noise(i)
        for i in range(4, 8):
            scale_noise_g(i)
        for i in range(4):
            project(1, (1,), i)
        turn_x(1, 6)
        for i in range(2):
            turn_back(1, i, False)
        turn_x(1, 7)
        for i in range(4, 6):
            turn_back(0, i, True)
        for i in range(4):
            project(1, (2,), i)
        for i in range(2):
            add_bias(1, (1,), i, "s")
        take_x(1, 6, "s")
        for i in range(2, 4):
            add_bias(1, (1,), i, "s")
        take_x(1, 7, "s")
        for i in range(4, 6):
            take_masked(i)
        for i in range(4):
            add_bias(1, (2,), i, "s")
        for i in range(2):
            fuse(i)
        amax_pad(0, 0, 0, 512)
        quantize_x(1, 3)
        amax_pad(1, 0, 512, 1024)
        store_out0(0)
        for i in range(4, 6):
            add_noise_g(i)
        for i in range(2, 4):
            turn_back(1, i, False)
        for i in range(6, 8):
            turn_back(0, i, True)
        for i in range(2):
            project(1, (3,), i)
        for i in range(4, 6):
            turn_back(1, i, False)
        for i in range(2, 4):
            project(1, (3,), i)
        take_masked(6)
        add_bias(1, (3,), 0, "s")
        take_masked(7)
        for i in range(1, 4):
            add_bias(1, (3,), i, "s")
        for i in range(2, 4):
            fuse(i)
        amax_pad(2, 1, 0, 512)
        amax_pad(3, 1, 512, 1024)
        for i in range(4, 6):
            fuse(i)
        amax_pad(4, 2, 0, 512)
        amax_pad(5, 2, 512, 1024)
        for i in range(1, 3):
            store_out0(i)
        for i in range(6, 8):
            add_noise_g(i)
        for i in range(6, 8):
            turn_back(1, i, False)
        for i in range(6, 8):
            fuse(i)
        amax_col(1, 3, 0, 512)
        amax_col(0, 3, 512, 1032)
        store_out0(3)
        spread_amax()
        cast_factor()
        for i in range(2):
            cast(i, 0, 1024, "v")
        cast(3, 0, 512, "v")
        for i in range(2):
            store_out1(i)
        cast(2, 0, 512, "s")
        for i in range(2, 4):
            cast(i, 512, 1024, "s")
        for i in range(2, 4):
            store_out1(i)
